import numpy as np
import ml_dtypes


def mxq(x, axis, fmt="e4m3"):
    dtype, down = {"e4m3": (ml_dtypes.float8_e4m3fn, 7), "e5m2": (ml_dtypes.float8_e5m2, 14)}[fmt]
    v = np.moveaxis(np.asarray(x, np.float32).astype(ml_dtypes.bfloat16).astype(np.float64), axis, -1)
    blocks = v.reshape(v.shape[:-1] + (-1, 32))
    amax = np.abs(blocks).max(-1, keepdims=True)
    byte = np.maximum(np.where(amax > 0, np.frexp(amax)[1] - 1 + 127, 0) - down, 1)
    scale = np.exp2(byte - 127.0)
    codes = (blocks / scale).astype(np.float32).astype(dtype).astype(np.float64)
    return np.moveaxis((codes * scale).reshape(v.shape), -1, axis)


WIDE = False


def mx_kscale(k):
    if not WIDE:
        return np.ones(k)
    levels = np.array([10, -10, 5, -5, 0])
    a = np.random.permutation(np.resize(levels, k // 512 * 4)).reshape(k // 512, 4)
    idx = np.arange(k)
    return np.exp2(a[idx // 512, idx % 128 // 32])


BF16 = ml_dtypes.bfloat16


def bf(x):
    return np.asarray(x, np.float32).astype(BF16)


def f64(x):
    return np.asarray(x).astype(np.float64)


E2M1 = np.array([0.0, 0.5, 1.0, 1.5, 2.0, 3.0, 4.0, 6.0, -0.0, -0.5, -1.0, -1.5, -2.0, -3.0, -4.0, -6.0])


def pack_weight(w, fmt):
    k, n = w.shape
    w = f64(bf(w)).reshape(k // 32, 32, n)
    amax = np.abs(w).max(1)
    if fmt == "e4m3":
        byte = np.frexp(amax)[1] - 1 + 127 - 7
    else:
        mant, ex = np.frexp(amax / 6.0)
        byte = np.where(mant > 0.5, ex, ex - 1) + 127
    byte = np.clip(np.where(amax > 0, byte, 1), 1, 254)
    scaled = (w * np.exp2(127.0 - byte)[:, None, :]).reshape(k, n).astype(np.float32)
    by_word = np.ascontiguousarray(scaled.reshape(k // 512, 128, 4, n).transpose(0, 1, 3, 2))
    if fmt == "e4m3":
        words = by_word.astype(ml_dtypes.float8_e4m3fn).view(np.uint8)
    else:
        c = by_word.astype(ml_dtypes.float4_e2m1fn).view(np.uint8) & 0xF
        words = c[..., 0::2] | (c[..., 1::2] << 4)
    return np.ascontiguousarray(words), np.ascontiguousarray(byte.astype(np.uint8).reshape(k // 512, 16, n))


def unpack_weight(words, scales, fmt):
    g, p, n, _ = words.shape
    if fmt == "e4m3":
        vals = np.ascontiguousarray(words).view(ml_dtypes.float8_e4m3fn).astype(np.float64)
    else:
        nib = np.empty((g, p, n, 4), np.uint8)
        nib[..., 0::2] = words & 0xF
        nib[..., 1::2] = words >> 4
        vals = E2M1[nib]
    vals = vals * np.repeat(np.exp2(scales.astype(np.float64) - 127.0), 8, axis=1)[..., None]
    return vals.transpose(0, 1, 3, 2).reshape(g * 512, n)


B, G, C, D, E, S = 2, 4, 512, 512, 1024, 128
N = G * C


def setup_inputs():
    t = np.exp2(np.round(np.log2(mx_kscale(C)) * 0.5))
    r = mx_kscale(E)
    q_quad = bf(np.random.standard_normal((B, G, C, S)) * 0.57 / S ** 0.25)
    k_quad = bf(np.random.standard_normal((B, G, C, S)) * 0.57 / S ** 0.25 * t[:, None])
    q_lin = bf(np.random.standard_normal((B, G, C, S)) / np.sqrt(S))
    kv = bf(np.random.standard_normal((B, S, E)) * 0.15 * np.sqrt(N))
    v = bf(np.tanh(np.random.standard_normal((B, G, C, E))) / (t * t)[:, None])
    u = bf(np.tanh(np.random.standard_normal((B, G, C, E))) * r)
    rel_bias = bf(np.random.standard_normal(C) * 0.2 * t)
    Wod_words, Wod_scales = pack_weight(np.random.standard_normal((E, D)) * 0.5 / np.sqrt(E) / r[:, None], "e4m3")
    bod = bf(np.random.standard_normal(D) * 0.3)
    return {"q_quad": q_quad,
            "k_quad": k_quad,
            "q_lin": q_lin,
            "kv": kv,
            "v": v,
            "u": u,
            "rel_bias": rel_bias,
            "Wod_words": Wod_words,
            "Wod_scales": Wod_scales,
            "bod": bod}


def reference(q_quad, k_quad, q_lin, kv, v, u, rel_bias, Wod_words, Wod_scales, bod):
    qk = f64(q_quad) @ f64(k_quad).transpose(0, 1, 3, 2)
    a = np.square(np.maximum(qk + f64(rel_bias), 0.0))
    v_quad = mxq(a, 3, "e4m3") @ mxq(f64(v), 2, "e4m3")
    v_lin = (f64(q_lin).reshape(B, N, S) @ f64(kv)).reshape(B, G, C, E)
    h = f64(u) * (v_quad + v_lin)
    return (mxq(h, 3, "e4m3") @ unpack_weight(Wod_words, Wod_scales, "e4m3")) + f64(bod)

@@ -1,0 +1,314 @@
+from contextlib import ExitStack
+
+import concourse.masks as masks
+import concourse.mybir as mybir
+
+BF16 = mybir.dt.bfloat16
+F32 = mybir.dt.float32
+I32 = mybir.dt.int32
+U32 = mybir.dt.uint32
+U8 = mybir.dt.uint8
+FP8X4 = mybir.dt.float8_e4m3fn_x4
+ACT = mybir.ActivationFunctionType
+ALU = mybir.AluOpType
+
+B, G, C, S, E, D = 2, 4, 512, 128, 1024, 512
+CHUNKS = B * G
+P = 128
+PACK = 4
+K_PASS = P * PACK
+SETS = C // P
+HALVES = E // K_PASS
+PAIR = 2
+
+FLOPS = 2 * CHUNKS * (C * C * S + C * C * E + C * S * E + C * E * D)
+
+
+def tile_flashattention_pa_t_kernel(
+    tc, q_quad, k_quad, q_lin, kv, v, u, rel_bias, Wod_words, Wod_scales, bod, out
+):
+    nc = tc.nc
+    with ExitStack() as pools:
+        const = pools.enter_context(tc.tile_pool(name="const", bufs=1))
+        loads = pools.enter_context(tc.tile_pool(name="loads", bufs=2))
+        work = pools.enter_context(tc.tile_pool(name="work", bufs=2))
+        psum = pools.enter_context(tc.psum_pool(name="psum", bufs=2))
+
+        tokens_in, values_in, gate_in = {}, {}, {}
+        keys_queries_T, lin_queries_T = {}, {}
+        relu_scores, scores_grouped, scores_mx = {}, {}, {}
+        values_grouped, values_mx = {}, {}
+        gate_T, v_sum, hidden_mx = {}, {}, {}
+
+        def load_tokens(c):
+            if c >= CHUNKS:
+                return
+            b, g = divmod(c, G)
+            tok = loads.tile([P, 3, SETS, S], BF16, tag="tokens", bufs=3)
+            for i, src in enumerate((k_quad, q_quad, q_lin)):
+                nc.sync.dma_start(out=tok[:, i], in_=src[b, g].rearrange("(p j) s -> p j s", j=SETS))
+            tokens_in[c] = tok
+
+        def load_values(c):
+            if c >= CHUNKS:
+                return
+            b, g = divmod(c, G)
+            val = loads.tile([P, PACK, E], BF16, tag="values")
+            nc.sync.dma_start(out=val[:], in_=v[b, g].rearrange("(p t) e -> p t e", t=PACK))
+            values_in[c] = val
+
+        def load_gate(c):
+            if c >= CHUNKS:
+                return
+            b, g = divmod(c, G)
+            gat = loads.tile([P, SETS, E], BF16, tag="gate")
+            nc.sync.dma_start(out=gat[:], in_=u[b, g].rearrange("(p j) e -> p j e", j=SETS))
+            gate_in[c] = gat
+
+        def transpose_tokens(c):
+            if c >= CHUNKS:
+                return
+            tok = tokens_in[c]
+            kq_ps = psum.tile([P, 2 * SETS, P], BF16, tag="misc")
+            for i in range(2):
+                for j in range(SETS):
+                    nc.tensor.transpose(kq_ps[:, i * SETS + j, :], tok[:, i, j, :], ident_bf[:])
+            kq = work.tile([P, 2 * SETS, P], BF16, tag="kqT")
+            nc.scalar.copy(out=kq[:], in_=kq_ps[:])
+            keys_queries_T[c] = kq
+            lin_ps = psum.tile([P, SETS, P], BF16, tag="misc")
+            for j in range(SETS):
+                nc.tensor.transpose(lin_ps[:, j, :], tok[:, 2, j, :], ident_bf[:])
+            lin = work.tile([P, SETS, P], BF16, tag="linT", bufs=3)
+            nc.scalar.copy(out=lin[:], in_=lin_ps[:])
+            lin_queries_T[c] = lin
+
+        def score_tile(c, t):
+            if c >= CHUNKS:
+                return
+            if t == 0:
+                relu_scores[c] = work.tile([P, PACK, C], F32, tag="relu", bufs=1, name="relu")
+            kq = keys_queries_T[c]
+            qk_ps = psum.tile([P, C], F32, tag="misc")
+            nc.tensor.matmul(
+                out=qk_ps[:],
+                lhsT=kq[:, t, :],
+                rhs=kq[:, SETS : 2 * SETS, :].rearrange("s j p -> s (j p)"),
+                start=True,
+                stop=True,
+            )
+            nc.scalar.activation(
+                out=relu_scores[c][:, t, :], in_=qk_ps[:], func=ACT.Relu, bias=key_bias[:, t : t + 1], scale=1.0
+            )
+
+        def square_piece(c, j):
+            if c >= CHUNKS:
+                return
+            if j == 0:
+                scores_grouped[c] = work.tile([P, C, PACK], BF16, tag="a_grp", bufs=1, align_bytes=64, name="a_grp")
+            cols = slice(j * P, (j + 1) * P)
+            nc.scalar.activation(
+                out=scores_grouped[c][:, cols, :],
+                in_=relu_scores[c][:, :, cols].rearrange("p t q -> p q t"),
+                func=ACT.Square,
+            )
+
+        def quantise_scores(c):
+            if c >= CHUNKS:
+                return
+            codes = work.tile([P, C], U32, tag="a_codes", align_bytes=64)
+            scales = work.tile([P, C], U8, tag="a_scales", align_bytes=64)
+            nc.vector.quantize_mx(
+                out=codes[:].bitcast(FP8X4),
+                scales=scales[:],
+                in_=scores_grouped[c][:].rearrange("p q t -> p (q t)"),
+            )
+            scores_mx[c] = (codes, scales)
+
+        def regroup_values(c):
+            if c >= CHUNKS:
+                return
+            grouped = work.tile([P, HALVES, PACK, P, PACK], BF16, tag="v_grp", bufs=1, align_bytes=64)
+            for half in range(HALVES):
+                nc.gpsimd.tensor_scalar(
+                    out=grouped[:, half].rearrange("p lane i t -> p i t lane"),
+                    in0=values_in[c][:, :, half * K_PASS : (half + 1) * K_PASS].rearrange(
+                        "p t (i lane) -> p i t lane", lane=PACK
+                    ),
+                    scalar1=1.0,
+                    scalar2=0.0,
+                    op0=ALU.mult,
+                    op1=ALU.add,
+                )
+            values_grouped[c] = grouped
+
+        def quantise_values(c):
+            if c >= CHUNKS:
+                return
+            codes = work.tile([P, HALVES, PACK, P], U32, tag="v_codes", align_bytes=64)
+            scales = work.tile([P, HALVES, PACK, P], U8, tag="v_scales", align_bytes=64)
+            nc.vector.quantize_mx(
+                out=codes[:].rearrange("p half lane i -> p (half lane i)").bitcast(FP8X4),
+                scales=scales[:].rearrange("p half lane i -> p (half lane i)"),
+                in_=values_grouped[c][:].rearrange("p half lane i t -> p (half lane i t)"),
+            )
+            values_mx[c] = (codes, scales)
+
+        def mix(c, half, lane):
+            b = c // G
+            if lane == 0:
+                v_sum[c, half] = work.tile([P, PACK, C], F32, tag="v_sum", name="v_sum")
+            total = v_sum[c, half][:, lane, :]
+            lin_ps = psum.tile([P, C], F32, tag="v_lin")
+            nc.tensor.matmul(
+                out=lin_ps[:],
+                lhsT=kv_sorted[:, b, half, lane, :],
+                rhs=lin_queries_T[c][:].rearrange("s j p -> s (j p)"),
+                start=True,
+                stop=True,
+            )
+            v_codes, v_scales = values_mx[c]
+            a_codes, a_scales = scores_mx[c]
+            quad_ps = psum.tile([P, C], F32, tag="v_quad")
+            nc.tensor.matmul_mx(
+                out=quad_ps[:],
+                lhsT=v_codes[:, half, lane, :].bitcast(FP8X4),
+                lhsT_scale=v_scales[:, half, lane, :],
+                rhs=a_codes[:].bitcast(FP8X4),
+                rhs_scale=a_scales[:],
+                start=True,
+                stop=True,
+            )
+            nc.scalar.copy(out=total, in_=lin_ps[:])
+            nc.vector.tensor_tensor(out=total, in0=quad_ps[:], in1=total, op=ALU.add)
+
+        def transpose_gate(c, half):
+            banks = []
+            for first_set in range(0, SETS, 2):
+                bank = psum.tile([P, PAIR, 2, P], F32, tag="gate_T")
+                for w in range(PAIR):
+                    for jj in range(2):
+                        words = gate_in[c][:, first_set + jj, :].bitcast(F32)
+                        first = half * (K_PASS // PAIR) + w
+                        last = (half + 1) * (K_PASS // PAIR)
+                        nc.tensor.transpose(bank[:, w, jj, :], words[:, first:last:PAIR], ident_f32[:])
+                banks.append(bank)
+            gate_T[c, half] = banks
+
+        def gate(c, half):
+            if half == 0:
+                codes = work.tile([P, HALVES, C], U32, tag="h_codes", align_bytes=64)
+                scales = work.tile([P, HALVES, C], U8, tag="h_scales", align_bytes=64)
+                hidden_mx[c] = (codes, scales)
+            codes, scales = hidden_mx[c]
+            grouped = work.tile([P, C, PACK], BF16, tag="h_grp", align_bytes=64)
+            for n, bank in enumerate(gate_T[c, half]):
+                cols = slice(n * 2 * P, (n + 1) * 2 * P)
+                nc.vector.tensor_tensor(
+                    out=grouped[:, cols, :].rearrange("p q (w e) -> p q w e", e=PAIR),
+                    in0=v_sum[c, half][:, :, cols].rearrange("p (w e) q -> p q w e", e=PAIR),
+                    in1=bank[:].bitcast(BF16).rearrange("p w j (i e) -> p (j i) w e", e=PAIR),
+                    op=ALU.mult,
+                )
+            nc.vector.quantize_mx(
+                out=codes[:, half, :].bitcast(FP8X4),
+                scales=scales[:, half, :],
+                in_=grouped[:].rearrange("p q t -> p (q t)"),
+            )
+
+        def project(c):
+            if c < 0:
+                return
+            b, g = divmod(c, G)
+            codes, scales = hidden_mx[c]
+            result = work.tile([P, SETS, D], F32, tag="result")
+            for j in range(SETS):
+                cols = slice(j * P, (j + 1) * P)
+                out_ps = psum.tile([P, D], F32, tag="misc")
+                for half in range(HALVES):
+                    nc.tensor.matmul_mx(
+                        out=out_ps[:],
+                        lhsT=codes[:, half, cols].bitcast(FP8X4),
+                        lhsT_scale=scales[:, half, cols],
+                        rhs=w_codes[:, half, :].bitcast(FP8X4),
+                        rhs_scale=w_scales[:, half, :],
+                        start=(half == 0),
+                        stop=(half == HALVES - 1),
+                    )
+                nc.vector.tensor_tensor(out=result[:, j, :], in0=out_ps[:], in1=bod_rows[:], op=ALU.add)
+            nc.sync.dma_start(out=out[b, g].rearrange("(p j) d -> p j d", j=SETS), in_=result[:])
+
+        ident_bf = const.tile([P, P], BF16)
+        masks.make_identity(nc, ident_bf[:])
+        ident_f32 = const.tile([P, P], F32)
+        masks.make_identity(nc, ident_f32[:])
+
+        bias_bf = const.tile([P, PACK], BF16)
+        nc.sync.dma_start(out=bias_bf[:], in_=rel_bias.rearrange("(p t) -> p t", t=PACK))
+        key_bias = const.tile([P, PACK], F32)
+        nc.vector.tensor_copy(out=key_bias[:], in_=bias_bf[:])
+
+        load_tokens(0)
+        load_values(0)
+        kv_in = const.tile([P, B, E], BF16)
+        nc.sync.dma_start(out=kv_in[:], in_=kv.rearrange("b s e -> s b e"))
+        load_tokens(1)
+        load_gate(0)
+
+        w_codes = const.tile([P, HALVES, D], U32, align_bytes=64)
+        nc.sync.dma_start(
+            out=w_codes[:].bitcast(I32), in_=Wod_words.rearrange("half p n t -> p half (n t)").bitcast(I32)
+        )
+        w_scales = const.tile([P, HALVES, D], U8, align_bytes=64)
+        nc.vector.memset(w_scales[:].bitcast(I32), 0)
+        for quadrant in range(4):
+            nc.sync.dma_start(
+                out=w_scales[32 * quadrant : 32 * quadrant + 4].bitcast(I32),
+                in_=Wod_scales[:, 4 * quadrant : 4 * quadrant + 4, :].rearrange("half r n -> r half n").bitcast(I32),
+            )
+        bod_bf = const.tile([P, D], BF16)
+        nc.sync.dma_start(out=bod_bf[:], in_=bod.partition_broadcast(P))
+        bod_rows = const.tile([P, D], F32)
+        nc.vector.tensor_copy(out=bod_rows[:], in_=bod_bf[:])
+        load_values(1)
+        load_tokens(2)
+
+        kv_sorted = const.tile([P, B, HALVES, PACK, P], BF16)
+        for b in range(B):
+            nc.vector.tensor_copy(
+                out=kv_sorted[:, b],
+                in_=kv_in[:, b, :].rearrange("s (half i lane) -> s half lane i", half=HALVES, lane=PACK),
+            )
+
+        transpose_tokens(0)
+        regroup_values(0)
+        for t in range(PACK):
+            score_tile(0, t)
+        transpose_tokens(1)
+        for j in range(SETS):
+            square_piece(0, j)
+        quantise_values(0)
+        quantise_scores(0)
+
+        for c in range(CHUNKS):
+            load_values(c + 2)
+            load_gate(c + 1)
+            load_tokens(c + 3)
+            regroup_values(c + 1)
+
+            for lane in range(PACK):
+                mix(c, 0, lane)
+                score_tile(c + 1, lane)
+            project(c - 1)
+            transpose_gate(c, 0)
+            gate(c, 0)
+
+            for lane in range(PACK):
+                mix(c, 1, lane)
+                square_piece(c + 1, lane)
+            transpose_gate(c, 1)
+            transpose_tokens(c + 2)
+            quantise_values(c + 1)
+            quantise_scores(c + 1)
+            gate(c, 1)
+        project(CHUNKS - 1)

@@ -131,9 +131,9 @@ def tile_flashattention_pa_t_kernel(
             grouped = work.tile([P, HALVES, PACK, P, PACK], BF16, tag="v_grp", bufs=1, align_bytes=64)
             for half in range(HALVES):
                 nc.gpsimd.tensor_scalar(
-                    out=grouped[:, half].rearrange("p lane i t -> p i t lane"),
+                    out=grouped[:, half],
                     in0=values_in[c][:, :, half * K_PASS : (half + 1) * K_PASS].rearrange(
-                        "p t (i lane) -> p i t lane", lane=PACK
+                        "p t (i lane) -> p lane i t", lane=PACK
                     ),
                     scalar1=1.0,
                     scalar2=0.0,

@@ -125,22 +125,19 @@ def tile_flashattention_pa_t_kernel(
             )
             scores_mx[c] = (codes, scales)
 
-        def regroup_values(c):
+        def regroup_values(c, half, lane, copy):
             if c >= CHUNKS:
                 return
-            grouped = work.tile([P, HALVES, PACK, P, PACK], BF16, tag="v_grp", bufs=1, align_bytes=64)
-            for half in range(HALVES):
-                nc.gpsimd.tensor_scalar(
-                    out=grouped[:, half],
-                    in0=values_in[c][:, :, half * K_PASS : (half + 1) * K_PASS].rearrange(
-                        "p t (i lane) -> p lane i t", lane=PACK
-                    ),
-                    scalar1=1.0,
-                    scalar2=0.0,
-                    op0=ALU.mult,
-                    op1=ALU.add,
+            if half == 0 and lane == 0:
+                values_grouped[c] = work.tile(
+                    [P, HALVES, PACK, P, PACK], BF16, tag="v_grp", bufs=1, align_bytes=64, name="v_grp"
                 )
-            values_grouped[c] = grouped
+            first = half * K_PASS + lane
+            last = (half + 1) * K_PASS
+            copy(
+                out=values_grouped[c][:, half, lane],
+                in_=values_in[c][:, :, first:last:PACK].rearrange("p t i -> p i t"),
+            )
 
         def quantise_values(c):
             if c >= CHUNKS:
@@ -281,7 +278,9 @@ def tile_flashattention_pa_t_kernel(
             )
 
         transpose_tokens(0)
-        regroup_values(0)
+        for half in range(HALVES):
+            for lane in range(PACK):
+                regroup_values(0, half, lane, nc.vector.tensor_copy)
         for t in range(PACK):
             score_tile(0, t)
         transpose_tokens(1)
@@ -294,11 +293,11 @@ def tile_flashattention_pa_t_kernel(
             load_values(c + 2)
             load_gate(c + 1)
             load_tokens(c + 3)
-            regroup_values(c + 1)
 
             for lane in range(PACK):
                 mix(c, 0, lane)
                 score_tile(c + 1, lane)
+                regroup_values(c + 1, 0, lane, nc.scalar.copy)
             project(c - 1)
             transpose_gate(c, 0)
             gate(c, 0)
@@ -306,6 +305,7 @@ def tile_flashattention_pa_t_kernel(
             for lane in range(PACK):
                 mix(c, 1, lane)
                 square_piece(c + 1, lane)
+                regroup_values(c + 1, 1, lane, nc.scalar.copy)
             transpose_gate(c, 1)
             transpose_tokens(c + 2)
             quantise_values(c + 1)

@@ -23,6 +23,26 @@ PAIR = 2
 
 FLOPS = 2 * CHUNKS * (C * C * S + C * C * E + C * S * E + C * E * D)
 
+SLOTS_PER_CHUNK = HALVES * PACK
+SLOTS = CHUNKS * SLOTS_PER_CHUNK
+TOKENS_LEAD = 15
+SCORES_LEAD = 12
+QUANT_SCORES_LEAD = 11
+REGROUP_LEAD = 8
+QUANT_VALUES_LEAD = 6
+LIN_LEAD = 2
+GATE_T_LAG = 2
+GATE_LAG = 4
+QUANT_HIDDEN_LAG = 4
+PROJECT_LAG = 12
+SCALAR_LANES = 3
+
+
+def place(m):
+    c, rest = divmod(m, SLOTS_PER_CHUNK)
+    half, lane = divmod(rest, PACK)
+    return c, half, lane
+
 
 def tile_flashattention_pa_t_kernel(
     tc, q_quad, k_quad, q_lin, kv, v, u, rel_bias, Wod_words, Wod_scales, bod, out
@@ -30,21 +50,22 @@ def tile_flashattention_pa_t_kernel(
     nc = tc.nc
     with ExitStack() as pools:
         const = pools.enter_context(tc.tile_pool(name="const", bufs=1))
-        loads = pools.enter_context(tc.tile_pool(name="loads", bufs=2))
+        loads = pools.enter_context(tc.tile_pool(name="loads", bufs=3))
         work = pools.enter_context(tc.tile_pool(name="work", bufs=2))
         psum = pools.enter_context(tc.psum_pool(name="psum", bufs=2))
+        pools.enter_context(tc.manual_schedule())
 
         tokens_in, values_in, gate_in = {}, {}, {}
         keys_queries_T, lin_queries_T = {}, {}
         relu_scores, scores_grouped, scores_mx = {}, {}, {}
         values_grouped, values_mx = {}, {}
-        gate_T, v_sum, hidden_mx = {}, {}, {}
+        gate_T, v_sum, hidden_grouped, hidden_mx = {}, {}, {}, {}
 
         def load_tokens(c):
             if c >= CHUNKS:
                 return
             b, g = divmod(c, G)
-            tok = loads.tile([P, 3, SETS, S], BF16, tag="tokens", bufs=3)
+            tok = loads.tile([P, 3, SETS, S], BF16, tag="tokens")
             for i, src in enumerate((k_quad, q_quad, q_lin)):
                 nc.sync.dma_start(out=tok[:, i], in_=src[b, g].rearrange("(p j) s -> p j s", j=SETS))
             tokens_in[c] = tok
@@ -65,8 +86,9 @@ def tile_flashattention_pa_t_kernel(
             nc.sync.dma_start(out=gat[:], in_=u[b, g].rearrange("(p j) e -> p j e", j=SETS))
             gate_in[c] = gat
 
-        def transpose_tokens(c):
-            if c >= CHUNKS:
+        def transpose_tokens(m):
+            c, half, lane = place(m)
+            if not 0 <= m < SLOTS or half != 0 or lane != 0:
                 return
             tok = tokens_in[c]
             kq_ps = psum.tile([P, 2 * SETS, P], BF16, tag="misc")
@@ -83,38 +105,42 @@ def tile_flashattention_pa_t_kernel(
             nc.scalar.copy(out=lin[:], in_=lin_ps[:])
             lin_queries_T[c] = lin
 
-        def score_tile(c, t):
-            if c >= CHUNKS:
+        def scores(m):
+            c, half, lane = place(m)
+            if not 0 <= m < SLOTS:
                 return
-            if t == 0:
-                relu_scores[c] = work.tile([P, PACK, C], F32, tag="relu", bufs=1, name="relu")
-            kq = keys_queries_T[c]
-            qk_ps = psum.tile([P, C], F32, tag="misc")
-            nc.tensor.matmul(
-                out=qk_ps[:],
-                lhsT=kq[:, t, :],
-                rhs=kq[:, SETS : 2 * SETS, :].rearrange("s j p -> s (j p)"),
-                start=True,
-                stop=True,
-            )
-            nc.scalar.activation(
-                out=relu_scores[c][:, t, :], in_=qk_ps[:], func=ACT.Relu, bias=key_bias[:, t : t + 1], scale=1.0
-            )
+            if half == 0:
+                if lane == 0:
+                    relu_scores[c] = work.tile([P, PACK, C], F32, tag="relu", bufs=1, name="relu")
+                kq = keys_queries_T[c]
+                qk_ps = psum.tile([P, C], F32, tag="misc")
+                nc.tensor.matmul(
+                    out=qk_ps[:],
+                    lhsT=kq[:, lane, :],
+                    rhs=kq[:, SETS : 2 * SETS, :].rearrange("s j p -> s (j p)"),
+                    start=True,
+                    stop=True,
+                )
+                nc.scalar.activation(
+                    out=relu_scores[c][:, lane, :],
+                    in_=qk_ps[:],
+                    func=ACT.Relu,
+                    bias=key_bias[:, lane : lane + 1],
+                    scale=1.0,
+                )
+            else:
+                if lane == 0:
+                    scores_grouped[c] = work.tile([P, C, PACK], BF16, tag="a_grp", align_bytes=64, name="a_grp")
+                cols = slice(lane * P, (lane + 1) * P)
+                nc.scalar.activation(
+                    out=scores_grouped[c][:, cols, :],
+                    in_=relu_scores[c][:, :, cols].rearrange("p t q -> p q t"),
+                    func=ACT.Square,
+                )
 
-        def square_piece(c, j):
-            if c >= CHUNKS:
-                return
-            if j == 0:
-                scores_grouped[c] = work.tile([P, C, PACK], BF16, tag="a_grp", bufs=1, align_bytes=64, name="a_grp")
-            cols = slice(j * P, (j + 1) * P)
-            nc.scalar.activation(
-                out=scores_grouped[c][:, cols, :],
-                in_=relu_scores[c][:, :, cols].rearrange("p t q -> p q t"),
-                func=ACT.Square,
-            )
-
-        def quantise_scores(c):
-            if c >= CHUNKS:
+        def quantise_scores(m):
+            c, half, lane = place(m)
+            if not 0 <= m < SLOTS or half != HALVES - 1 or lane != PACK - 1:
                 return
             codes = work.tile([P, C], U32, tag="a_codes", align_bytes=64)
             scales = work.tile([P, C], U8, tag="a_scales", align_bytes=64)
@@ -125,115 +151,131 @@ def tile_flashattention_pa_t_kernel(
             )
             scores_mx[c] = (codes, scales)
 
-        def regroup_values(c, half, lane, copy):
-            if c >= CHUNKS:
+        def regroup_values(m, vector_is_idle):
+            c, half, lane = place(m)
+            if not 0 <= m < SLOTS:
                 return
-            if half == 0 and lane == 0:
-                values_grouped[c] = work.tile(
-                    [P, HALVES, PACK, P, PACK], BF16, tag="v_grp", bufs=1, align_bytes=64, name="v_grp"
-                )
+            copy = nc.scalar.copy if lane < SCALAR_LANES and not vector_is_idle else nc.vector.tensor_copy
+            if lane == 0:
+                values_grouped[c, half] = work.tile([P, PACK, P, PACK], BF16, tag="v_grp", align_bytes=64, name="v_grp")
             first = half * K_PASS + lane
             last = (half + 1) * K_PASS
             copy(
-                out=values_grouped[c][:, half, lane],
+                out=values_grouped[c, half][:, lane],
                 in_=values_in[c][:, :, first:last:PACK].rearrange("p t i -> p i t"),
             )
 
-        def quantise_values(c):
-            if c >= CHUNKS:
+        def quantise_values(m):
+            c, half, lane = place(m)
+            if not 0 <= m < SLOTS or lane != PACK - 1:
                 return
-            codes = work.tile([P, HALVES, PACK, P], U32, tag="v_codes", align_bytes=64)
-            scales = work.tile([P, HALVES, PACK, P], U8, tag="v_scales", align_bytes=64)
+            codes = work.tile([P, PACK, P], U32, tag="v_codes", bufs=3, align_bytes=64)
+            scales = work.tile([P, PACK, P], U8, tag="v_scales", bufs=3, align_bytes=64)
             nc.vector.quantize_mx(
-                out=codes[:].rearrange("p half lane i -> p (half lane i)").bitcast(FP8X4),
-                scales=scales[:].rearrange("p half lane i -> p (half lane i)"),
-                in_=values_grouped[c][:].rearrange("p half lane i t -> p (half lane i t)"),
+                out=codes[:].rearrange("p lane i -> p (lane i)").bitcast(FP8X4),
+                scales=scales[:].rearrange("p lane i -> p (lane i)"),
+                in_=values_grouped[c, half][:].rearrange("p lane i t -> p (lane i t)"),
             )
-            values_mx[c] = (codes, scales)
+            values_mx[c, half] = (codes, scales)
 
-        def mix(c, half, lane):
-            b = c // G
+        def linear_attention(m):
+            c, half, lane = place(m)
+            if not 0 <= m < SLOTS:
+                return
             if lane == 0:
-                v_sum[c, half] = work.tile([P, PACK, C], F32, tag="v_sum", name="v_sum")
-            total = v_sum[c, half][:, lane, :]
+                v_sum[c, half] = work.tile([P, PACK, C], F32, tag="v_sum", bufs=3, name="v_sum")
             lin_ps = psum.tile([P, C], F32, tag="v_lin")
             nc.tensor.matmul(
                 out=lin_ps[:],
-                lhsT=kv_sorted[:, b, half, lane, :],
+                lhsT=kv_sorted[:, c // G, half, lane, :],
                 rhs=lin_queries_T[c][:].rearrange("s j p -> s (j p)"),
                 start=True,
                 stop=True,
             )
-            v_codes, v_scales = values_mx[c]
+            nc.scalar.copy(out=v_sum[c, half][:, lane, :], in_=lin_ps[:])
+
+        def quadratic_attention(m):
+            c, half, lane = place(m)
+            if not 0 <= m < SLOTS:
+                return
+            v_codes, v_scales = values_mx[c, half]
             a_codes, a_scales = scores_mx[c]
             quad_ps = psum.tile([P, C], F32, tag="v_quad")
             nc.tensor.matmul_mx(
                 out=quad_ps[:],
-                lhsT=v_codes[:, half, lane, :].bitcast(FP8X4),
-                lhsT_scale=v_scales[:, half, lane, :],
+                lhsT=v_codes[:, lane, :].bitcast(FP8X4),
+                lhsT_scale=v_scales[:, lane, :],
                 rhs=a_codes[:].bitcast(FP8X4),
                 rhs_scale=a_scales[:],
                 start=True,
                 stop=True,
             )
-            nc.scalar.copy(out=total, in_=lin_ps[:])
+            total = v_sum[c, half][:, lane, :]
             nc.vector.tensor_tensor(out=total, in0=quad_ps[:], in1=total, op=ALU.add)
 
-        def transpose_gate(c, half):
-            banks = []
-            for first_set in range(0, SETS, 2):
-                bank = psum.tile([P, PAIR, 2, P], F32, tag="gate_T")
-                for w in range(PAIR):
-                    for jj in range(2):
-                        words = gate_in[c][:, first_set + jj, :].bitcast(F32)
-                        first = half * (K_PASS // PAIR) + w
-                        last = (half + 1) * (K_PASS // PAIR)
-                        nc.tensor.transpose(bank[:, w, jj, :], words[:, first:last:PAIR], ident_f32[:])
-                banks.append(bank)
-            gate_T[c, half] = banks
+        def transpose_gate(m):
+            c, half, lane = place(m)
+            if not 0 <= m < SLOTS or lane % 2 != 0:
+                return
+            bank = psum.tile([P, PAIR, 2, P], F32, tag="gate_T")
+            for w in range(PAIR):
+                for jj in range(2):
+                    words = gate_in[c][:, lane + jj, :].bitcast(F32)
+                    first = half * (K_PASS // PAIR) + w
+                    last = (half + 1) * (K_PASS // PAIR)
+                    nc.tensor.transpose(bank[:, w, jj, :], words[:, first:last:PAIR], ident_f32[:])
+            gate_T[c, half, lane] = bank
 
-        def gate(c, half):
+        def gate(m):
+            c, half, lane = place(m)
+            if not 0 <= m < SLOTS or lane % 2 != 0:
+                return
+            if lane == 0:
+                hidden_grouped[c, half] = work.tile([P, C, PACK], BF16, tag="h_grp", align_bytes=64, name="h_grp")
+            cols = slice(lane * P, (lane + 2) * P)
+            nc.vector.tensor_tensor(
+                out=hidden_grouped[c, half][:, cols, :].rearrange("p q (w e) -> p q w e", e=PAIR),
+                in0=v_sum[c, half][:, :, cols].rearrange("p (w e) q -> p q w e", e=PAIR),
+                in1=gate_T[c, half, lane][:].bitcast(BF16).rearrange("p w j (i e) -> p (j i) w e", e=PAIR),
+                op=ALU.mult,
+            )
+
+        def quantise_hidden(m):
+            c, half, lane = place(m)
+            if not 0 <= m < SLOTS or lane != PACK - 1:
+                return
             if half == 0:
                 codes = work.tile([P, HALVES, C], U32, tag="h_codes", align_bytes=64)
                 scales = work.tile([P, HALVES, C], U8, tag="h_scales", align_bytes=64)
                 hidden_mx[c] = (codes, scales)
             codes, scales = hidden_mx[c]
-            grouped = work.tile([P, C, PACK], BF16, tag="h_grp", align_bytes=64)
-            for n, bank in enumerate(gate_T[c, half]):
-                cols = slice(n * 2 * P, (n + 1) * 2 * P)
-                nc.vector.tensor_tensor(
-                    out=grouped[:, cols, :].rearrange("p q (w e) -> p q w e", e=PAIR),
-                    in0=v_sum[c, half][:, :, cols].rearrange("p (w e) q -> p q w e", e=PAIR),
-                    in1=bank[:].bitcast(BF16).rearrange("p w j (i e) -> p (j i) w e", e=PAIR),
-                    op=ALU.mult,
-                )
             nc.vector.quantize_mx(
                 out=codes[:, half, :].bitcast(FP8X4),
                 scales=scales[:, half, :],
-                in_=grouped[:].rearrange("p q t -> p (q t)"),
+                in_=hidden_grouped[c, half][:].rearrange("p q t -> p (q t)"),
             )
 
-        def project(c):
-            if c < 0:
+        def project(m):
+            c, half, j = place(m)
+            if not 0 <= m < SLOTS or half != HALVES - 1:
                 return
             b, g = divmod(c, G)
             codes, scales = hidden_mx[c]
-            result = work.tile([P, SETS, D], F32, tag="result")
-            for j in range(SETS):
-                cols = slice(j * P, (j + 1) * P)
-                out_ps = psum.tile([P, D], F32, tag="misc")
-                for half in range(HALVES):
-                    nc.tensor.matmul_mx(
-                        out=out_ps[:],
-                        lhsT=codes[:, half, cols].bitcast(FP8X4),
-                        lhsT_scale=scales[:, half, cols],
-                        rhs=w_codes[:, half, :].bitcast(FP8X4),
-                        rhs_scale=w_scales[:, half, :],
-                        start=(half == 0),
-                        stop=(half == HALVES - 1),
-                    )
-                nc.vector.tensor_tensor(out=result[:, j, :], in0=out_ps[:], in1=bod_rows[:], op=ALU.add)
-            nc.sync.dma_start(out=out[b, g].rearrange("(p j) d -> p j d", j=SETS), in_=result[:])
+            cols = slice(j * P, (j + 1) * P)
+            out_ps = psum.tile([P, D], F32, tag="misc")
+            for k_half in range(HALVES):
+                nc.tensor.matmul_mx(
+                    out=out_ps[:],
+                    lhsT=codes[:, k_half, cols].bitcast(FP8X4),
+                    lhsT_scale=scales[:, k_half, cols],
+                    rhs=w_codes[:, k_half, :].bitcast(FP8X4),
+                    rhs_scale=w_scales[:, k_half, :],
+                    start=(k_half == 0),
+                    stop=(k_half == HALVES - 1),
+                )
+            result = work.tile([P, D], F32, tag="result", bufs=4)
+            nc.vector.tensor_tensor(out=result[:], in0=out_ps[:], in1=bod_rows[:], op=ALU.add)
+            nc.sync.dma_start(out=out[b, g].rearrange("(p j) d -> p j d", j=SETS)[:, j, :], in_=result[:])
 
         ident_bf = const.tile([P, P], BF16)
         masks.make_identity(nc, ident_bf[:])
@@ -246,9 +288,9 @@ def tile_flashattention_pa_t_kernel(
         nc.vector.tensor_copy(out=key_bias[:], in_=bias_bf[:])
 
         load_tokens(0)
-        load_values(0)
         kv_in = const.tile([P, B, E], BF16)
         nc.sync.dma_start(out=kv_in[:], in_=kv.rearrange("b s e -> s b e"))
+        load_values(0)
         load_tokens(1)
         load_gate(0)
 
@@ -263,10 +305,8 @@ def tile_flashattention_pa_t_kernel(
                 out=w_scales[32 * quadrant : 32 * quadrant + 4].bitcast(I32),
                 in_=Wod_scales[:, 4 * quadrant : 4 * quadrant + 4, :].rearrange("half r n -> r half n").bitcast(I32),
             )
-        bod_bf = const.tile([P, D], BF16)
-        nc.sync.dma_start(out=bod_bf[:], in_=bod.partition_broadcast(P))
-        bod_rows = const.tile([P, D], F32)
-        nc.vector.tensor_copy(out=bod_rows[:], in_=bod_bf[:])
+        bod_rows = const.tile([P, D], BF16)
+        nc.sync.dma_start(out=bod_rows[:], in_=bod.partition_broadcast(P))
         load_values(1)
         load_tokens(2)
 
@@ -277,38 +317,20 @@ def tile_flashattention_pa_t_kernel(
                 in_=kv_in[:, b, :].rearrange("s (half i lane) -> s half lane i", half=HALVES, lane=PACK),
             )
 
-        transpose_tokens(0)
-        for half in range(HALVES):
-            for lane in range(PACK):
-                regroup_values(0, half, lane, nc.vector.tensor_copy)
-        for t in range(PACK):
-            score_tile(0, t)
-        transpose_tokens(1)
-        for j in range(SETS):
-            square_piece(0, j)
-        quantise_values(0)
-        quantise_scores(0)
-
-        for c in range(CHUNKS):
-            load_values(c + 2)
-            load_gate(c + 1)
-            load_tokens(c + 3)
-
-            for lane in range(PACK):
-                mix(c, 0, lane)
-                score_tile(c + 1, lane)
-                regroup_values(c + 1, 0, lane, nc.scalar.copy)
-            project(c - 1)
-            transpose_gate(c, 0)
-            gate(c, 0)
-
-            for lane in range(PACK):
-                mix(c, 1, lane)
-                square_piece(c + 1, lane)
-                regroup_values(c + 1, 1, lane, nc.scalar.copy)
-            transpose_gate(c, 1)
-            transpose_tokens(c + 2)
-            quantise_values(c + 1)
-            quantise_scores(c + 1)
-            gate(c, 1)
-        project(CHUNKS - 1)
+        for n in range(-TOKENS_LEAD, SLOTS + PROJECT_LAG):
+            if n >= 0 and n % SLOTS_PER_CHUNK == 0:
+                c = n // SLOTS_PER_CHUNK
+                load_gate(c + 1)
+                load_values(c + 2)
+                load_tokens(c + 3)
+            quadratic_attention(n)
+            gate(n - GATE_LAG)
+            linear_attention(n + LIN_LEAD)
+            scores(n + SCORES_LEAD)
+            regroup_values(n + REGROUP_LEAD, n < 0)
+            transpose_gate(n - GATE_T_LAG)
+            transpose_tokens(n + TOKENS_LEAD)
+            quantise_hidden(n - QUANT_HIDDEN_LAG)
+            quantise_scores(n + QUANT_SCORES_LEAD)
+            quantise_values(n + QUANT_VALUES_LEAD)
+            project(n - PROJECT_LAG)

@@ -23,25 +23,24 @@ PAIR = 2
 
 FLOPS = 2 * CHUNKS * (C * C * S + C * C * E + C * S * E + C * E * D)
 
-SLOTS_PER_CHUNK = HALVES * PACK
+SLOTS_PER_CHUNK = SETS * HALVES
 SLOTS = CHUNKS * SLOTS_PER_CHUNK
 TOKENS_LEAD = 15
-SCORES_LEAD = 12
+PREPARE_LEAD = 12
 QUANT_SCORES_LEAD = 11
-REGROUP_LEAD = 8
-QUANT_VALUES_LEAD = 6
+QUANT_VALUES_LEAD = 10
 LIN_LEAD = 2
-GATE_T_LAG = 2
-GATE_LAG = 4
-QUANT_HIDDEN_LAG = 4
-PROJECT_LAG = 12
+GATE_T_LEAD = 1
+GATE_LAG = 1
+QUANT_HIDDEN_LAG = 2
+PROJECT_LAG = 5
 SCALAR_LANES = 3
 
 
 def place(m):
-    c, rest = divmod(m, SLOTS_PER_CHUNK)
-    half, lane = divmod(rest, PACK)
-    return c, half, lane
+    c, piece = divmod(m, SLOTS_PER_CHUNK)
+    j, half = divmod(piece, HALVES)
+    return c, j, half
 
 
 def tile_flashattention_pa_t_kernel(
@@ -87,8 +86,8 @@ def tile_flashattention_pa_t_kernel(
             gate_in[c] = gat
 
         def transpose_tokens(m):
-            c, half, lane = place(m)
-            if not 0 <= m < SLOTS or half != 0 or lane != 0:
+            c, piece = divmod(m, SLOTS_PER_CHUNK)
+            if not 0 <= m < SLOTS or piece != 0:
                 return
             tok = tokens_in[c]
             kq_ps = psum.tile([P, 2 * SETS, P], BF16, tag="misc")
@@ -106,32 +105,30 @@ def tile_flashattention_pa_t_kernel(
             lin_queries_T[c] = lin
 
         def scores(m):
-            c, half, lane = place(m)
+            c, piece = divmod(m, SLOTS_PER_CHUNK)
             if not 0 <= m < SLOTS:
                 return
-            if half == 0:
-                if lane == 0:
+            if piece < PACK:
+                t = piece
+                if t == 0:
                     relu_scores[c] = work.tile([P, PACK, C], F32, tag="relu", bufs=1, name="relu")
                 kq = keys_queries_T[c]
                 qk_ps = psum.tile([P, C], F32, tag="misc")
                 nc.tensor.matmul(
                     out=qk_ps[:],
-                    lhsT=kq[:, lane, :],
+                    lhsT=kq[:, t, :],
                     rhs=kq[:, SETS : 2 * SETS, :].rearrange("s j p -> s (j p)"),
                     start=True,
                     stop=True,
                 )
                 nc.scalar.activation(
-                    out=relu_scores[c][:, lane, :],
-                    in_=qk_ps[:],
-                    func=ACT.Relu,
-                    bias=key_bias[:, lane : lane + 1],
-                    scale=1.0,
+                    out=relu_scores[c][:, t, :], in_=qk_ps[:], func=ACT.Relu, bias=key_bias[:, t : t + 1], scale=1.0
                 )
             else:
-                if lane == 0:
+                j = piece - PACK
+                if j == 0:
                     scores_grouped[c] = work.tile([P, C, PACK], BF16, tag="a_grp", align_bytes=64, name="a_grp")
-                cols = slice(lane * P, (lane + 1) * P)
+                cols = slice(j * P, (j + 1) * P)
                 nc.scalar.activation(
                     out=scores_grouped[c][:, cols, :],
                     in_=relu_scores[c][:, :, cols].rearrange("p t q -> p q t"),
@@ -139,8 +136,8 @@ def tile_flashattention_pa_t_kernel(
                 )
 
         def quantise_scores(m):
-            c, half, lane = place(m)
-            if not 0 <= m < SLOTS or half != HALVES - 1 or lane != PACK - 1:
+            c, piece = divmod(m, SLOTS_PER_CHUNK)
+            if not 0 <= m < SLOTS or piece != SLOTS_PER_CHUNK - 1:
                 return
             codes = work.tile([P, C], U32, tag="a_codes", align_bytes=64)
             scales = work.tile([P, C], U8, tag="a_scales", align_bytes=64)
@@ -151,123 +148,129 @@ def tile_flashattention_pa_t_kernel(
             )
             scores_mx[c] = (codes, scales)
 
-        def regroup_values(m, vector_is_idle):
-            c, half, lane = place(m)
+        def regroup_values(m):
+            c, piece = divmod(m, SLOTS_PER_CHUNK)
             if not 0 <= m < SLOTS:
                 return
-            copy = nc.scalar.copy if lane < SCALAR_LANES and not vector_is_idle else nc.vector.tensor_copy
-            if lane == 0:
-                values_grouped[c, half] = work.tile([P, PACK, P, PACK], BF16, tag="v_grp", align_bytes=64, name="v_grp")
+            half, lane = divmod(piece, PACK)
+            copy = nc.scalar.copy if lane < SCALAR_LANES and c > 0 else nc.vector.tensor_copy
+            if piece == 0:
+                values_grouped[c] = work.tile(
+                    [P, HALVES, PACK, P, PACK], BF16, tag="v_grp", align_bytes=64, name="v_grp"
+                )
             first = half * K_PASS + lane
             last = (half + 1) * K_PASS
             copy(
-                out=values_grouped[c, half][:, lane],
+                out=values_grouped[c][:, half, lane],
                 in_=values_in[c][:, :, first:last:PACK].rearrange("p t i -> p i t"),
             )
 
         def quantise_values(m):
-            c, half, lane = place(m)
+            c, piece = divmod(m, SLOTS_PER_CHUNK)
+            half, lane = divmod(piece, PACK)
             if not 0 <= m < SLOTS or lane != PACK - 1:
                 return
-            codes = work.tile([P, PACK, P], U32, tag="v_codes", bufs=3, align_bytes=64)
-            scales = work.tile([P, PACK, P], U8, tag="v_scales", bufs=3, align_bytes=64)
+            if half == 0:
+                codes = work.tile([P, HALVES, PACK, P], U32, tag="v_codes", align_bytes=64)
+                scales = work.tile([P, HALVES, PACK, P], U8, tag="v_scales", align_bytes=64)
+                values_mx[c] = (codes, scales)
+            codes, scales = values_mx[c]
             nc.vector.quantize_mx(
-                out=codes[:].rearrange("p lane i -> p (lane i)").bitcast(FP8X4),
-                scales=scales[:].rearrange("p lane i -> p (lane i)"),
-                in_=values_grouped[c, half][:].rearrange("p lane i t -> p (lane i t)"),
+                out=codes[:, half].rearrange("p lane i -> p (lane i)").bitcast(FP8X4),
+                scales=scales[:, half].rearrange("p lane i -> p (lane i)"),
+                in_=values_grouped[c][:, half].rearrange("p lane i t -> p (lane i t)"),
             )
-            values_mx[c, half] = (codes, scales)
 
         def linear_attention(m):
-            c, half, lane = place(m)
+            c, j, half = place(m)
             if not 0 <= m < SLOTS:
                 return
-            if lane == 0:
-                v_sum[c, half] = work.tile([P, PACK, C], F32, tag="v_sum", bufs=3, name="v_sum")
-            lin_ps = psum.tile([P, C], F32, tag="v_lin")
-            nc.tensor.matmul(
-                out=lin_ps[:],
-                lhsT=kv_sorted[:, c // G, half, lane, :],
-                rhs=lin_queries_T[c][:].rearrange("s j p -> s (j p)"),
-                start=True,
-                stop=True,
-            )
-            nc.scalar.copy(out=v_sum[c, half][:, lane, :], in_=lin_ps[:])
+            lin_ps = psum.tile([P, PACK, P], F32, tag="v_lin")
+            for lane in range(PACK):
+                nc.tensor.matmul(
+                    out=lin_ps[:, lane, :],
+                    lhsT=kv_sorted[:, c // G, half, lane, :],
+                    rhs=lin_queries_T[c][:, j, :],
+                    start=True,
+                    stop=True,
+                )
+            total = work.tile([P, P, PACK], F32, tag="v_sum", bufs=6)
+            nc.scalar.copy(out=total[:], in_=lin_ps[:].rearrange("p lane q -> p q lane"))
+            v_sum[m] = total
 
         def quadratic_attention(m):
-            c, half, lane = place(m)
+            c, j, half = place(m)
             if not 0 <= m < SLOTS:
                 return
-            v_codes, v_scales = values_mx[c, half]
+            v_codes, v_scales = values_mx[c]
             a_codes, a_scales = scores_mx[c]
-            quad_ps = psum.tile([P, C], F32, tag="v_quad")
-            nc.tensor.matmul_mx(
-                out=quad_ps[:],
-                lhsT=v_codes[:, lane, :].bitcast(FP8X4),
-                lhsT_scale=v_scales[:, lane, :],
-                rhs=a_codes[:].bitcast(FP8X4),
-                rhs_scale=a_scales[:],
-                start=True,
-                stop=True,
+            cols = slice(j * P, (j + 1) * P)
+            quad_ps = psum.tile([P, PACK, P], F32, tag="v_quad")
+            for lane in range(PACK):
+                nc.tensor.matmul_mx(
+                    out=quad_ps[:, lane, :],
+                    lhsT=v_codes[:, half, lane, :].bitcast(FP8X4),
+                    lhsT_scale=v_scales[:, half, lane, :],
+                    rhs=a_codes[:, cols].bitcast(FP8X4),
+                    rhs_scale=a_scales[:, cols],
+                    start=True,
+                    stop=True,
+                )
+            nc.vector.tensor_tensor(
+                out=v_sum[m][:], in0=quad_ps[:].rearrange("p lane q -> p q lane"), in1=v_sum[m][:], op=ALU.add
             )
-            total = v_sum[c, half][:, lane, :]
-            nc.vector.tensor_tensor(out=total, in0=quad_ps[:], in1=total, op=ALU.add)
 
         def transpose_gate(m):
-            c, half, lane = place(m)
-            if not 0 <= m < SLOTS or lane % 2 != 0:
+            c, j, half = place(m)
+            if not 0 <= m < SLOTS or half != 0:
                 return
-            bank = psum.tile([P, PAIR, 2, P], F32, tag="gate_T")
-            for w in range(PAIR):
-                for jj in range(2):
-                    words = gate_in[c][:, lane + jj, :].bitcast(F32)
-                    first = half * (K_PASS // PAIR) + w
-                    last = (half + 1) * (K_PASS // PAIR)
-                    nc.tensor.transpose(bank[:, w, jj, :], words[:, first:last:PAIR], ident_f32[:])
-            gate_T[c, half, lane] = bank
+            words = gate_in[c][:, j, :].bitcast(F32)
+            bank = psum.tile([P, HALVES, PAIR, P], F32, tag="gate_T")
+            for k_half in range(HALVES):
+                for w in range(PAIR):
+                    first = k_half * (K_PASS // PAIR) + w
+                    last = (k_half + 1) * (K_PASS // PAIR)
+                    nc.tensor.transpose(bank[:, k_half, w, :], words[:, first:last:PAIR], ident_f32[:])
+            gate_T[c, j] = bank
 
         def gate(m):
-            c, half, lane = place(m)
-            if not 0 <= m < SLOTS or lane % 2 != 0:
+            c, j, half = place(m)
+            if not 0 <= m < SLOTS:
                 return
-            if lane == 0:
-                hidden_grouped[c, half] = work.tile([P, C, PACK], BF16, tag="h_grp", align_bytes=64, name="h_grp")
-            cols = slice(lane * P, (lane + 2) * P)
+            if half == 0:
+                hidden_grouped[c, j] = work.tile([P, HALVES, P, PACK], BF16, tag="h_grp", align_bytes=64, name="h_grp")
             nc.vector.tensor_tensor(
-                out=hidden_grouped[c, half][:, cols, :].rearrange("p q (w e) -> p q w e", e=PAIR),
-                in0=v_sum[c, half][:, :, cols].rearrange("p (w e) q -> p q w e", e=PAIR),
-                in1=gate_T[c, half, lane][:].bitcast(BF16).rearrange("p w j (i e) -> p (j i) w e", e=PAIR),
+                out=hidden_grouped[c, j][:, half].rearrange("p q (w e) -> p q w e", e=PAIR),
+                in0=v_sum[m][:].rearrange("p q (w e) -> p q w e", e=PAIR),
+                in1=gate_T[c, j][:, half].bitcast(BF16).rearrange("p w (q e) -> p q w e", e=PAIR),
                 op=ALU.mult,
             )
 
         def quantise_hidden(m):
-            c, half, lane = place(m)
-            if not 0 <= m < SLOTS or lane != PACK - 1:
+            c, j, half = place(m)
+            if not 0 <= m < SLOTS or half != HALVES - 1:
                 return
-            if half == 0:
-                codes = work.tile([P, HALVES, C], U32, tag="h_codes", align_bytes=64)
-                scales = work.tile([P, HALVES, C], U8, tag="h_scales", align_bytes=64)
-                hidden_mx[c] = (codes, scales)
-            codes, scales = hidden_mx[c]
+            codes = work.tile([P, HALVES, P], U32, tag="h_codes", align_bytes=64)
+            scales = work.tile([P, HALVES, P], U8, tag="h_scales", align_bytes=64)
             nc.vector.quantize_mx(
-                out=codes[:, half, :].bitcast(FP8X4),
-                scales=scales[:, half, :],
-                in_=hidden_grouped[c, half][:].rearrange("p q t -> p (q t)"),
+                out=codes[:].rearrange("p half q -> p (half q)").bitcast(FP8X4),
+                scales=scales[:].rearrange("p half q -> p (half q)"),
+                in_=hidden_grouped[c, j][:].rearrange("p half q t -> p (half q t)"),
             )
+            hidden_mx[c, j] = (codes, scales)
 
         def project(m):
-            c, half, j = place(m)
+            c, j, half = place(m)
             if not 0 <= m < SLOTS or half != HALVES - 1:
                 return
             b, g = divmod(c, G)
-            codes, scales = hidden_mx[c]
-            cols = slice(j * P, (j + 1) * P)
+            codes, scales = hidden_mx[c, j]
             out_ps = psum.tile([P, D], F32, tag="misc")
             for k_half in range(HALVES):
                 nc.tensor.matmul_mx(
                     out=out_ps[:],
-                    lhsT=codes[:, k_half, cols].bitcast(FP8X4),
-                    lhsT_scale=scales[:, k_half, cols],
+                    lhsT=codes[:, k_half, :].bitcast(FP8X4),
+                    lhsT_scale=scales[:, k_half, :],
                     rhs=w_codes[:, k_half, :].bitcast(FP8X4),
                     rhs_scale=w_scales[:, k_half, :],
                     start=(k_half == 0),
@@ -292,6 +295,7 @@ def tile_flashattention_pa_t_kernel(
         nc.sync.dma_start(out=kv_in[:], in_=kv.rearrange("b s e -> s b e"))
         load_values(0)
         load_tokens(1)
+        load_values(1)
         load_gate(0)
 
         w_codes = const.tile([P, HALVES, D], U32, align_bytes=64)
@@ -307,8 +311,8 @@ def tile_flashattention_pa_t_kernel(
             )
         bod_rows = const.tile([P, D], BF16)
         nc.sync.dma_start(out=bod_rows[:], in_=bod.partition_broadcast(P))
-        load_values(1)
         load_tokens(2)
+        load_values(2)
 
         kv_sorted = const.tile([P, B, HALVES, PACK, P], BF16)
         for b in range(B):
@@ -321,16 +325,16 @@ def tile_flashattention_pa_t_kernel(
             if n >= 0 and n % SLOTS_PER_CHUNK == 0:
                 c = n // SLOTS_PER_CHUNK
                 load_gate(c + 1)
-                load_values(c + 2)
                 load_tokens(c + 3)
+                load_values(c + 3)
             quadratic_attention(n)
             gate(n - GATE_LAG)
+            project(n - PROJECT_LAG)
             linear_attention(n + LIN_LEAD)
-            scores(n + SCORES_LEAD)
-            regroup_values(n + REGROUP_LEAD, n < 0)
-            transpose_gate(n - GATE_T_LAG)
+            scores(n + PREPARE_LEAD)
+            regroup_values(n + PREPARE_LEAD)
+            transpose_gate(n + GATE_T_LEAD)
             transpose_tokens(n + TOKENS_LEAD)
             quantise_hidden(n - QUANT_HIDDEN_LAG)
             quantise_scores(n + QUANT_SCORES_LEAD)
             quantise_values(n + QUANT_VALUES_LEAD)
-            project(n - PROJECT_LAG)

@@ -34,7 +34,6 @@ GATE_T_LEAD = 1
 GATE_LAG = 1
 QUANT_HIDDEN_LAG = 2
 PROJECT_LAG = 5
-SCALAR_LANES = 3
 
 
 def place(m):
@@ -153,17 +152,18 @@ def tile_flashattention_pa_t_kernel(
             if not 0 <= m < SLOTS:
                 return
             half, lane = divmod(piece, PACK)
-            copy = nc.scalar.copy if lane < SCALAR_LANES and c > 0 else nc.vector.tensor_copy
             if piece == 0:
                 values_grouped[c] = work.tile(
                     [P, HALVES, PACK, P, PACK], BF16, tag="v_grp", align_bytes=64, name="v_grp"
                 )
             first = half * K_PASS + lane
             last = (half + 1) * K_PASS
-            copy(
-                out=values_grouped[c][:, half, lane],
-                in_=values_in[c][:, :, first:last:PACK].rearrange("p t i -> p i t"),
-            )
+            grouped = values_grouped[c][:, half, lane]
+            rows = values_in[c][:, :, first:last:PACK].rearrange("p t i -> p i t")
+            if c > 0:
+                nc.gpsimd.tensor_scalar(out=grouped, in0=rows, scalar1=1.0, scalar2=0.0, op0=ALU.mult, op1=ALU.add)
+            else:
+                nc.vector.tensor_copy(out=grouped, in_=rows)
 
         def quantise_values(m):
             c, piece = divmod(m, SLOTS_PER_CHUNK)

@@ -34,6 +34,7 @@ GATE_T_LEAD = 1
 GATE_LAG = 1
 QUANT_HIDDEN_LAG = 2
 PROJECT_LAG = 5
+STORE_LAG = 6
 
 
 def place(m):
@@ -57,7 +58,7 @@ def tile_flashattention_pa_t_kernel(
         keys_queries_T, lin_queries_T = {}, {}
         relu_scores, scores_grouped, scores_mx = {}, {}, {}
         values_grouped, values_mx = {}, {}
-        gate_T, v_sum, hidden_grouped, hidden_mx = {}, {}, {}, {}
+        gate_T, v_sum, hidden_grouped, hidden_mx, projected = {}, {}, {}, {}, {}
 
         def load_tokens(c):
             if c >= CHUNKS:
@@ -263,7 +264,6 @@ def tile_flashattention_pa_t_kernel(
             c, j, half = place(m)
             if not 0 <= m < SLOTS or half != HALVES - 1:
                 return
-            b, g = divmod(c, G)
             codes, scales = hidden_mx[c, j]
             out_ps = psum.tile([P, D], F32, tag="misc")
             for k_half in range(HALVES):
@@ -276,8 +276,17 @@ def tile_flashattention_pa_t_kernel(
                     start=(k_half == 0),
                     stop=(k_half == HALVES - 1),
                 )
+            product = work.tile([P, D], F32, tag="product", bufs=3)
+            nc.scalar.copy(out=product[:], in_=out_ps[:])
+            projected[c, j] = product
+
+        def add_bias_and_store(m):
+            c, j, half = place(m)
+            if not 0 <= m < SLOTS or half != HALVES - 1:
+                return
+            b, g = divmod(c, G)
             result = work.tile([P, D], F32, tag="result", bufs=4)
-            nc.vector.tensor_tensor(out=result[:], in0=out_ps[:], in1=bod_rows[:], op=ALU.add)
+            nc.gpsimd.tensor_tensor(out=result[:], in0=projected[c, j][:], in1=bod_rows[:], op=ALU.add)
             nc.sync.dma_start(out=out[b, g].rearrange("(p j) d -> p j d", j=SETS)[:, j, :], in_=result[:])
 
         ident_bf = const.tile([P, P], BF16)
@@ -321,7 +330,7 @@ def tile_flashattention_pa_t_kernel(
                 in_=kv_in[:, b, :].rearrange("s (half i lane) -> s half lane i", half=HALVES, lane=PACK),
             )
 
-        for n in range(-TOKENS_LEAD, SLOTS + PROJECT_LAG):
+        for n in range(-TOKENS_LEAD, SLOTS + STORE_LAG):
             if n >= 0 and n % SLOTS_PER_CHUNK == 0:
                 c = n // SLOTS_PER_CHUNK
                 load_gate(c + 1)
@@ -330,6 +339,7 @@ def tile_flashattention_pa_t_kernel(
             quadratic_attention(n)
             gate(n - GATE_LAG)
             project(n - PROJECT_LAG)
+            add_bias_and_store(n - STORE_LAG)
             linear_attention(n + LIN_LEAD)
             scores(n + PREPARE_LEAD)
             regroup_values(n + PREPARE_LEAD)

@@ -27,8 +27,10 @@ SLOTS_PER_CHUNK = SETS * HALVES
 SLOTS = CHUNKS * SLOTS_PER_CHUNK
 TOKENS_LEAD = 15
 PREPARE_LEAD = 12
-QUANT_SCORES_LEAD = 11
-QUANT_VALUES_LEAD = 10
+QUANT_SCORES_LEAD = 10
+QUANT_VALUES_LEAD = 9
+REGROUP_LEAD = 11
+LANES_AT_ONCE = 2
 LIN_LEAD = 2
 GATE_T_LEAD = 1
 GATE_LAG = 1
@@ -150,36 +152,36 @@ def tile_flashattention_pa_t_kernel(
 
         def regroup_values(m):
             c, piece = divmod(m, SLOTS_PER_CHUNK)
-            if not 0 <= m < SLOTS:
+            if not 0 <= m < SLOTS or piece % LANES_AT_ONCE != 0:
                 return
             half, lane = divmod(piece, PACK)
-            if piece == 0:
-                values_grouped[c] = work.tile(
-                    [P, HALVES, PACK, P, PACK], BF16, tag="v_grp", align_bytes=64, name="v_grp"
-                )
-            first = half * K_PASS + lane
-            last = (half + 1) * K_PASS
-            grouped = values_grouped[c][:, half, lane]
-            rows = values_in[c][:, :, first:last:PACK].rearrange("p t i -> p i t")
+            grouped = work.tile([P, LANES_AT_ONCE, P, PACK], BF16, tag="v_grp", bufs=1, align_bytes=64)
+            rows = values_in[c][:, :, half * K_PASS : (half + 1) * K_PASS].rearrange(
+                "p t (i lane) -> p lane i t", lane=PACK
+            )[:, lane : lane + LANES_AT_ONCE]
             if c > 0:
-                nc.gpsimd.tensor_scalar(out=grouped, in0=rows, scalar1=1.0, scalar2=0.0, op0=ALU.mult, op1=ALU.add)
+                nc.gpsimd.tensor_scalar(
+                    out=grouped[:], in0=rows, scalar1=1.0, scalar2=0.0, op0=ALU.mult, op1=ALU.add
+                )
             else:
-                nc.vector.tensor_copy(out=grouped, in_=rows)
+                nc.vector.tensor_copy(out=grouped[:], in_=rows)
+            values_grouped[c, piece] = grouped
 
         def quantise_values(m):
             c, piece = divmod(m, SLOTS_PER_CHUNK)
-            half, lane = divmod(piece, PACK)
-            if not 0 <= m < SLOTS or lane != PACK - 1:
+            if not 0 <= m < SLOTS or piece % LANES_AT_ONCE != 0:
                 return
-            if half == 0:
+            half, lane = divmod(piece, PACK)
+            if piece == 0:
                 codes = work.tile([P, HALVES, PACK, P], U32, tag="v_codes", align_bytes=64)
                 scales = work.tile([P, HALVES, PACK, P], U8, tag="v_scales", align_bytes=64)
                 values_mx[c] = (codes, scales)
             codes, scales = values_mx[c]
+            lanes = slice(lane, lane + LANES_AT_ONCE)
             nc.vector.quantize_mx(
-                out=codes[:, half].rearrange("p lane i -> p (lane i)").bitcast(FP8X4),
-                scales=scales[:, half].rearrange("p lane i -> p (lane i)"),
-                in_=values_grouped[c][:, half].rearrange("p lane i t -> p (lane i t)"),
+                out=codes[:, half, lanes].rearrange("p lane i -> p (lane i)").bitcast(FP8X4),
+                scales=scales[:, half, lanes].rearrange("p lane i -> p (lane i)"),
+                in_=values_grouped[c, piece][:].rearrange("p lane i t -> p (lane i t)"),
             )
 
         def linear_attention(m):
@@ -339,12 +341,12 @@ def tile_flashattention_pa_t_kernel(
             quadratic_attention(n)
             gate(n - GATE_LAG)
             project(n - PROJECT_LAG)
-            add_bias_and_store(n - STORE_LAG)
             linear_attention(n + LIN_LEAD)
             scores(n + PREPARE_LEAD)
-            regroup_values(n + PREPARE_LEAD)
             transpose_gate(n + GATE_T_LEAD)
             transpose_tokens(n + TOKENS_LEAD)
             quantise_hidden(n - QUANT_HIDDEN_LAG)
-            quantise_scores(n + QUANT_SCORES_LEAD)
             quantise_values(n + QUANT_VALUES_LEAD)
+            quantise_scores(n + QUANT_SCORES_LEAD)
+            regroup_values(n + REGROUP_LEAD)
+            add_bias_and_store(n - STORE_LAG)

@@ -220,7 +220,7 @@ def tile_flashattention_pa_t_kernel(
                     stop=True,
                 )
             nc.vector.tensor_tensor(
-                out=v_sum[m][:], in0=quad_ps[:].rearrange("p lane q -> p q lane"), in1=v_sum[m][:], op=ALU.add
+                out=v_sum[m][:], in0=v_sum[m][:], in1=quad_ps[:].rearrange("p lane q -> p q lane"), op=ALU.add
             )
 
         def transpose_gate(m):

@@ -262,6 +262,10 @@ def tile_flashattention_pa_t_kernel(
             )
             hidden_mx[c, j] = (codes, scales)
 
+        def out_rows(c, j):
+            b, g = divmod(c, G)
+            return out[b, g].rearrange("(p j) d -> p j d", j=SETS)[:, j, :]
+
         def project(m):
             c, j, half = place(m)
             if not 0 <= m < SLOTS or half != HALVES - 1:
@@ -278,18 +282,24 @@ def tile_flashattention_pa_t_kernel(
                     start=(k_half == 0),
                     stop=(k_half == HALVES - 1),
                 )
-            product = work.tile([P, D], F32, tag="product", bufs=3)
-            nc.scalar.copy(out=product[:], in_=out_ps[:])
-            projected[c, j] = product
+            result = work.tile([P, D], F32, tag="result", bufs=4)
+            if j % 2 == 1:
+                nc.vector.tensor_tensor(out=result[:], in0=out_ps[:], in1=bod_rows[:], op=ALU.add)
+                nc.sync.dma_start(out=out_rows(c, j), in_=result[:])
+            else:
+                product = work.tile([P, D], F32, tag="product", bufs=3)
+                nc.scalar.copy(out=product[:], in_=out_ps[:])
+                projected[c, j] = (result, product)
 
         def add_bias_and_store(m):
             c, j, half = place(m)
             if not 0 <= m < SLOTS or half != HALVES - 1:
                 return
-            b, g = divmod(c, G)
-            result = work.tile([P, D], F32, tag="result", bufs=4)
-            nc.gpsimd.tensor_tensor(out=result[:], in0=projected[c, j][:], in1=bod_rows[:], op=ALU.add)
-            nc.sync.dma_start(out=out[b, g].rearrange("(p j) d -> p j d", j=SETS)[:, j, :], in_=result[:])
+            part = j % 2
+            result, product = projected[c, j - part]
+            cols = slice(part * (D // 2), (part + 1) * (D // 2))
+            nc.gpsimd.tensor_tensor(out=result[:, cols], in0=product[:, cols], in1=bod_rows[:, cols], op=ALU.add)
+            nc.sync.dma_start(out=out_rows(c, j - part)[:, cols], in_=result[:, cols])
 
         ident_bf = const.tile([P, P], BF16)
         masks.make_identity(nc, ident_bf[:])

@@ -31,8 +31,8 @@ QUANT_SCORES_LEAD = 10
 QUANT_VALUES_LEAD = 9
 REGROUP_LEAD = 11
 LANES_AT_ONCE = 2
-LIN_LEAD = 2
-GATE_T_LEAD = 1
+LIN_LEAD = 3
+GATE_T_LAG = 1
 GATE_LAG = 1
 QUANT_HIDDEN_LAG = 2
 PROJECT_LAG = 5
@@ -110,6 +110,7 @@ def tile_flashattention_pa_t_kernel(
             c, piece = divmod(m, SLOTS_PER_CHUNK)
             if not 0 <= m < SLOTS:
                 return
+            on_vector = m < PREPARE_LEAD and piece % 2 == 1
             if piece < PACK:
                 t = piece
                 if t == 0:
@@ -123,19 +124,31 @@ def tile_flashattention_pa_t_kernel(
                     start=True,
                     stop=True,
                 )
-                nc.scalar.activation(
-                    out=relu_scores[c][:, t, :], in_=qk_ps[:], func=ACT.Relu, bias=key_bias[:, t : t + 1], scale=1.0
-                )
+                if on_vector:
+                    nc.vector.tensor_scalar(
+                        out=relu_scores[c][:, t, :],
+                        in0=qk_ps[:],
+                        scalar1=key_bias[:, t : t + 1],
+                        scalar2=0.0,
+                        op0=ALU.add,
+                        op1=ALU.max,
+                    )
+                else:
+                    nc.scalar.activation(
+                        out=relu_scores[c][:, t, :], in_=qk_ps[:], func=ACT.Relu, bias=key_bias[:, t : t + 1], scale=1.0
+                    )
             else:
                 j = piece - PACK
                 if j == 0:
                     scores_grouped[c] = work.tile([P, C, PACK], BF16, tag="a_grp", align_bytes=64, name="a_grp")
                 cols = slice(j * P, (j + 1) * P)
-                nc.scalar.activation(
-                    out=scores_grouped[c][:, cols, :],
-                    in_=relu_scores[c][:, :, cols].rearrange("p t q -> p q t"),
-                    func=ACT.Square,
-                )
+                relu_grouped = relu_scores[c][:, :, cols].rearrange("p t q -> p q t")
+                if on_vector:
+                    nc.vector.tensor_tensor(
+                        out=scores_grouped[c][:, cols, :], in0=relu_grouped, in1=relu_grouped, op=ALU.mult
+                    )
+                else:
+                    nc.scalar.activation(out=scores_grouped[c][:, cols, :], in_=relu_grouped, func=ACT.Square)
 
         def quantise_scores(m):
             c, piece = divmod(m, SLOTS_PER_CHUNK)
@@ -197,9 +210,9 @@ def tile_flashattention_pa_t_kernel(
                     start=True,
                     stop=True,
                 )
-            total = work.tile([P, P, PACK], F32, tag="v_sum", bufs=6)
-            nc.scalar.copy(out=total[:], in_=lin_ps[:].rearrange("p lane q -> p q lane"))
-            v_sum[m] = total
+            if half == 0:
+                v_sum[c, j] = work.tile([P, HALVES, P, PACK], F32, tag="v_sum", bufs=4, name="v_sum")
+            nc.scalar.copy(out=v_sum[c, j][:, half], in_=lin_ps[:].rearrange("p lane q -> p q lane"))
 
         def quadratic_attention(m):
             c, j, half = place(m)
@@ -220,7 +233,10 @@ def tile_flashattention_pa_t_kernel(
                     stop=True,
                 )
             nc.vector.tensor_tensor(
-                out=v_sum[m][:], in0=v_sum[m][:], in1=quad_ps[:].rearrange("p lane q -> p q lane"), op=ALU.add
+                out=v_sum[c, j][:, half],
+                in0=v_sum[c, j][:, half],
+                in1=quad_ps[:].rearrange("p lane q -> p q lane"),
+                op=ALU.add,
             )
 
         def transpose_gate(m):
@@ -228,26 +244,26 @@ def tile_flashattention_pa_t_kernel(
             if not 0 <= m < SLOTS or half != 0:
                 return
             words = gate_in[c][:, j, :].bitcast(F32)
-            bank = psum.tile([P, HALVES, PAIR, P], F32, tag="gate_T")
+            bank = psum.tile([P, PAIR, HALVES, P], F32, tag="gate_T")
             for k_half in range(HALVES):
                 for w in range(PAIR):
                     first = k_half * (K_PASS // PAIR) + w
                     last = (k_half + 1) * (K_PASS // PAIR)
-                    nc.tensor.transpose(bank[:, k_half, w, :], words[:, first:last:PAIR], ident_f32[:])
+                    nc.tensor.transpose(bank[:, w, k_half, :], words[:, first:last:PAIR], ident_f32[:])
             gate_T[c, j] = bank
 
         def gate(m):
             c, j, half = place(m)
-            if not 0 <= m < SLOTS:
+            if not 0 <= m < SLOTS or half != HALVES - 1:
                 return
-            if half == 0:
-                hidden_grouped[c, j] = work.tile([P, HALVES, P, PACK], BF16, tag="h_grp", align_bytes=64, name="h_grp")
+            hidden = work.tile([P, HALVES, P, PACK], BF16, tag="h_grp", align_bytes=64)
             nc.vector.tensor_tensor(
-                out=hidden_grouped[c, j][:, half].rearrange("p q (w e) -> p q w e", e=PAIR),
-                in0=v_sum[m][:].rearrange("p q (w e) -> p q w e", e=PAIR),
-                in1=gate_T[c, j][:, half].bitcast(BF16).rearrange("p w (q e) -> p q w e", e=PAIR),
+                out=hidden[:].rearrange("p half q (w e) -> p (half q) w e", e=PAIR),
+                in0=v_sum[c, j][:].rearrange("p half q (w e) -> p (half q) w e", e=PAIR),
+                in1=gate_T[c, j][:].bitcast(BF16).rearrange("p w half (q e) -> p (half q) w e", e=PAIR),
                 op=ALU.mult,
             )
+            hidden_grouped[c, j] = hidden
 
         def quantise_hidden(m):
             c, j, half = place(m)
@@ -312,9 +328,9 @@ def tile_flashattention_pa_t_kernel(
         nc.vector.tensor_copy(out=key_bias[:], in_=bias_bf[:])
 
         load_tokens(0)
+        load_values(0)
         kv_in = const.tile([P, B, E], BF16)
         nc.sync.dma_start(out=kv_in[:], in_=kv.rearrange("b s e -> s b e"))
-        load_values(0)
         load_tokens(1)
         load_values(1)
         load_gate(0)
@@ -337,9 +353,13 @@ def tile_flashattention_pa_t_kernel(
 
         kv_sorted = const.tile([P, B, HALVES, PACK, P], BF16)
         for b in range(B):
-            nc.vector.tensor_copy(
+            nc.gpsimd.tensor_scalar(
                 out=kv_sorted[:, b],
-                in_=kv_in[:, b, :].rearrange("s (half i lane) -> s half lane i", half=HALVES, lane=PACK),
+                in0=kv_in[:, b, :].rearrange("s (half i lane) -> s half lane i", half=HALVES, lane=PACK),
+                scalar1=1.0,
+                scalar2=0.0,
+                op0=ALU.mult,
+                op1=ALU.add,
             )
 
         for n in range(-TOKENS_LEAD, SLOTS + STORE_LAG):
@@ -351,10 +371,13 @@ def tile_flashattention_pa_t_kernel(
             quadratic_attention(n)
             gate(n - GATE_LAG)
             project(n - PROJECT_LAG)
-            linear_attention(n + LIN_LEAD)
-            scores(n + PREPARE_LEAD)
-            transpose_gate(n + GATE_T_LEAD)
+            if (n + LIN_LEAD) % HALVES == 0:
+                linear_attention(n + LIN_LEAD)
+            transpose_gate(n - GATE_T_LAG)
             transpose_tokens(n + TOKENS_LEAD)
+            if (n + LIN_LEAD) % HALVES == 0:
+                linear_attention(n + LIN_LEAD + 1)
+            scores(n + PREPARE_LEAD)
             quantise_hidden(n - QUANT_HIDDEN_LAG)
             quantise_values(n + QUANT_VALUES_LEAD)
             quantise_scores(n + QUANT_SCORES_LEAD)

@@ -298,12 +298,12 @@ def tile_flashattention_pa_t_kernel(
                     start=(k_half == 0),
                     stop=(k_half == HALVES - 1),
                 )
-            result = work.tile([P, D], F32, tag="result", bufs=4)
+            result = work.tile([P, D], F32, tag="result", bufs=32)
             if j % 2 == 1:
                 nc.vector.tensor_tensor(out=result[:], in0=out_ps[:], in1=bod_rows[:], op=ALU.add)
                 nc.sync.dma_start(out=out_rows(c, j), in_=result[:])
             else:
-                product = work.tile([P, D], F32, tag="product", bufs=3)
+                product = work.tile([P, D], F32, tag="product", bufs=16)
                 nc.scalar.copy(out=product[:], in_=out_ps[:])
                 projected[c, j] = (result, product)
 

@@ -25,18 +25,17 @@ FLOPS = 2 * CHUNKS * (C * C * S + C * C * E + C * S * E + C * E * D)
 
 SLOTS_PER_CHUNK = SETS * HALVES
 SLOTS = CHUNKS * SLOTS_PER_CHUNK
-TOKENS_LEAD = 15
-PREPARE_LEAD = 12
-QUANT_SCORES_LEAD = 10
-QUANT_VALUES_LEAD = 9
-REGROUP_LEAD = 11
-LANES_AT_ONCE = 2
+PERIOD = 4
+RELU_BUFS = 2
+PRODUCT_BUFS = 4
+FIRST_SQUARES_ON_VECTOR = (1, 3)
+TOKENS_LEAD = 13
+PREPARE_LEAD = 11
 LIN_LEAD = 3
 GATE_T_LAG = 1
 GATE_LAG = 1
-QUANT_HIDDEN_LAG = 2
 PROJECT_LAG = 5
-STORE_LAG = 6
+FIRST_REGROUP = ("vector", "scalar", "vector", "vector")
 
 
 def place(m):
@@ -60,7 +59,7 @@ def tile_flashattention_pa_t_kernel(
         keys_queries_T, lin_queries_T = {}, {}
         relu_scores, scores_grouped, scores_mx = {}, {}, {}
         values_grouped, values_mx = {}, {}
-        gate_T, v_sum, hidden_grouped, hidden_mx, projected = {}, {}, {}, {}, {}
+        gate_T, v_sum, hidden_grouped, hidden_mx, products = {}, {}, {}, {}, {}
 
         def load_tokens(c):
             if c >= CHUNKS:
@@ -76,7 +75,13 @@ def tile_flashattention_pa_t_kernel(
                 return
             b, g = divmod(c, G)
             val = loads.tile([P, PACK, E], BF16, tag="values")
-            nc.sync.dma_start(out=val[:], in_=v[b, g].rearrange("(p t) e -> p t e", t=PACK))
+            rows = v[b, g].rearrange("(p t) e -> p t e", t=PACK)
+            if c == 0:
+                for half in range(HALVES):
+                    cols = slice(half * K_PASS, (half + 1) * K_PASS)
+                    nc.sync.dma_start(out=val[:, :, cols], in_=rows[:, :, cols])
+            else:
+                nc.sync.dma_start(out=val[:], in_=rows)
             values_in[c] = val
 
         def load_gate(c):
@@ -87,17 +92,27 @@ def tile_flashattention_pa_t_kernel(
             nc.sync.dma_start(out=gat[:], in_=u[b, g].rearrange("(p j) e -> p j e", j=SETS))
             gate_in[c] = gat
 
-        def transpose_tokens(m):
-            c, piece = divmod(m, SLOTS_PER_CHUNK)
-            if not 0 <= m < SLOTS or piece != 0:
+        def transpose_tokens(c):
+            if not 0 <= c < CHUNKS:
                 return
             tok = tokens_in[c]
-            kq_ps = psum.tile([P, 2 * SETS, P], BF16, tag="misc")
-            for i in range(2):
-                for j in range(SETS):
-                    nc.tensor.transpose(kq_ps[:, i * SETS + j, :], tok[:, i, j, :], ident_bf[:])
             kq = work.tile([P, 2 * SETS, P], BF16, tag="kqT")
-            nc.scalar.copy(out=kq[:], in_=kq_ps[:])
+            if c == 0:
+                for i in range(2):
+                    part_ps = psum.tile([P, SETS, P], BF16, tag="misc")
+                    for j in range(SETS):
+                        nc.tensor.transpose(part_ps[:, j, :], tok[:, i, j, :], ident_bf[:])
+                    part = kq[:, i * SETS : (i + 1) * SETS, :]
+                    if i == 0:
+                        nc.scalar.copy(out=part, in_=part_ps[:])
+                    else:
+                        nc.vector.tensor_copy(out=part, in_=part_ps[:])
+            else:
+                kq_ps = psum.tile([P, 2 * SETS, P], BF16, tag="misc")
+                for i in range(2):
+                    for j in range(SETS):
+                        nc.tensor.transpose(kq_ps[:, i * SETS + j, :], tok[:, i, j, :], ident_bf[:])
+                nc.scalar.copy(out=kq[:], in_=kq_ps[:])
             keys_queries_T[c] = kq
             lin_ps = psum.tile([P, SETS, P], BF16, tag="misc")
             for j in range(SETS):
@@ -106,95 +121,99 @@ def tile_flashattention_pa_t_kernel(
             nc.scalar.copy(out=lin[:], in_=lin_ps[:])
             lin_queries_T[c] = lin
 
+        def score_relu(c, t):
+            if t == 0:
+                relu_scores[c] = work.tile([P, PACK, C], F32, tag="relu", bufs=RELU_BUFS, name="relu")
+            kq = keys_queries_T[c]
+            qk_ps = psum.tile([P, C], F32, tag="misc")
+            nc.tensor.matmul(
+                out=qk_ps[:],
+                lhsT=kq[:, t, :],
+                rhs=kq[:, SETS : 2 * SETS, :].rearrange("s j p -> s (j p)"),
+                start=True,
+                stop=True,
+            )
+            if c == 0 and t % 2 == 1:
+                nc.vector.tensor_scalar(
+                    out=relu_scores[c][:, t, :],
+                    in0=qk_ps[:],
+                    scalar1=key_bias[:, t : t + 1],
+                    scalar2=0.0,
+                    op0=ALU.add,
+                    op1=ALU.max,
+                )
+            else:
+                nc.scalar.activation(
+                    out=relu_scores[c][:, t, :], in_=qk_ps[:], func=ACT.Relu, bias=key_bias[:, t : t + 1], scale=1.0
+                )
+
+        def score_square(c, j):
+            if j == 0:
+                scores_grouped[c] = work.tile([P, C, PACK], BF16, tag="a_grp", align_bytes=64, name="a_grp")
+            cols = slice(j * P, (j + 1) * P)
+            relu_grouped = relu_scores[c][:, :, cols].rearrange("p t q -> p q t")
+            if c == 0 and j in FIRST_SQUARES_ON_VECTOR:
+                nc.vector.tensor_tensor(
+                    out=scores_grouped[c][:, cols, :], in0=relu_grouped, in1=relu_grouped, op=ALU.mult
+                )
+            else:
+                nc.scalar.activation(out=scores_grouped[c][:, cols, :], in_=relu_grouped, func=ACT.Square)
+
         def scores(m):
             c, piece = divmod(m, SLOTS_PER_CHUNK)
-            if not 0 <= m < SLOTS:
+            if not 0 <= c < CHUNKS:
                 return
-            on_vector = m < PREPARE_LEAD and piece % 2 == 1
             if piece < PACK:
-                t = piece
-                if t == 0:
-                    relu_scores[c] = work.tile([P, PACK, C], F32, tag="relu", bufs=1, name="relu")
-                kq = keys_queries_T[c]
-                qk_ps = psum.tile([P, C], F32, tag="misc")
-                nc.tensor.matmul(
-                    out=qk_ps[:],
-                    lhsT=kq[:, t, :],
-                    rhs=kq[:, SETS : 2 * SETS, :].rearrange("s j p -> s (j p)"),
-                    start=True,
-                    stop=True,
-                )
-                if on_vector:
-                    nc.vector.tensor_scalar(
-                        out=relu_scores[c][:, t, :],
-                        in0=qk_ps[:],
-                        scalar1=key_bias[:, t : t + 1],
-                        scalar2=0.0,
-                        op0=ALU.add,
-                        op1=ALU.max,
-                    )
-                else:
-                    nc.scalar.activation(
-                        out=relu_scores[c][:, t, :], in_=qk_ps[:], func=ACT.Relu, bias=key_bias[:, t : t + 1], scale=1.0
-                    )
+                score_relu(c, piece)
             else:
-                j = piece - PACK
-                if j == 0:
-                    scores_grouped[c] = work.tile([P, C, PACK], BF16, tag="a_grp", align_bytes=64, name="a_grp")
-                cols = slice(j * P, (j + 1) * P)
-                relu_grouped = relu_scores[c][:, :, cols].rearrange("p t q -> p q t")
-                if on_vector:
-                    nc.vector.tensor_tensor(
-                        out=scores_grouped[c][:, cols, :], in0=relu_grouped, in1=relu_grouped, op=ALU.mult
-                    )
-                else:
-                    nc.scalar.activation(out=scores_grouped[c][:, cols, :], in_=relu_grouped, func=ACT.Square)
+                score_square(c, piece - PACK)
 
-        def quantise_scores(m):
-            c, piece = divmod(m, SLOTS_PER_CHUNK)
-            if not 0 <= m < SLOTS or piece != SLOTS_PER_CHUNK - 1:
+        def quantise_scores(c, pair):
+            if not 0 <= c < CHUNKS:
                 return
-            codes = work.tile([P, C], U32, tag="a_codes", align_bytes=64)
-            scales = work.tile([P, C], U8, tag="a_scales", align_bytes=64)
+            if pair == 0:
+                codes = work.tile([P, C], U32, tag="a_codes", align_bytes=64)
+                scales = work.tile([P, C], U8, tag="a_scales", align_bytes=64)
+                scores_mx[c] = (codes, scales)
+            codes, scales = scores_mx[c]
+            cols = slice(pair * 2 * P, (pair + 1) * 2 * P)
             nc.vector.quantize_mx(
-                out=codes[:].bitcast(FP8X4),
-                scales=scales[:],
-                in_=scores_grouped[c][:].rearrange("p q t -> p (q t)"),
+                out=codes[:, cols].bitcast(FP8X4),
+                scales=scales[:, cols],
+                in_=scores_grouped[c][:, cols].rearrange("p q t -> p (q t)"),
             )
-            scores_mx[c] = (codes, scales)
 
-        def regroup_values(m):
-            c, piece = divmod(m, SLOTS_PER_CHUNK)
-            if not 0 <= m < SLOTS or piece % LANES_AT_ONCE != 0:
+        def regroup_values(c, half, lane=0, lanes=PACK, who="gpsimd"):
+            if not 0 <= c < CHUNKS:
                 return
-            half, lane = divmod(piece, PACK)
-            grouped = work.tile([P, LANES_AT_ONCE, P, PACK], BF16, tag="v_grp", bufs=1, align_bytes=64)
+            tag = "v_grp_scalar" if who == "scalar" else "v_grp"
+            grouped = work.tile([P, lanes, P, PACK], BF16, tag=tag, bufs=1, align_bytes=64, name="v_grp")
             rows = values_in[c][:, :, half * K_PASS : (half + 1) * K_PASS].rearrange(
                 "p t (i lane) -> p lane i t", lane=PACK
-            )[:, lane : lane + LANES_AT_ONCE]
-            if c > 0:
+            )[:, lane : lane + lanes]
+            if who == "gpsimd":
                 nc.gpsimd.tensor_scalar(
                     out=grouped[:], in0=rows, scalar1=1.0, scalar2=0.0, op0=ALU.mult, op1=ALU.add
                 )
+            elif who == "scalar":
+                nc.scalar.copy(out=grouped[:], in_=rows)
             else:
                 nc.vector.tensor_copy(out=grouped[:], in_=rows)
-            values_grouped[c, piece] = grouped
+            values_grouped[c, half, lane] = grouped
 
-        def quantise_values(m):
-            c, piece = divmod(m, SLOTS_PER_CHUNK)
-            if not 0 <= m < SLOTS or piece % LANES_AT_ONCE != 0:
+        def quantise_values(c, half, lane=0, lanes=PACK):
+            if not 0 <= c < CHUNKS:
                 return
-            half, lane = divmod(piece, PACK)
-            if piece == 0:
+            if half == 0 and lane == 0:
                 codes = work.tile([P, HALVES, PACK, P], U32, tag="v_codes", align_bytes=64)
                 scales = work.tile([P, HALVES, PACK, P], U8, tag="v_scales", align_bytes=64)
                 values_mx[c] = (codes, scales)
             codes, scales = values_mx[c]
-            lanes = slice(lane, lane + LANES_AT_ONCE)
+            some = slice(lane, lane + lanes)
             nc.vector.quantize_mx(
-                out=codes[:, half, lanes].rearrange("p lane i -> p (lane i)").bitcast(FP8X4),
-                scales=scales[:, half, lanes].rearrange("p lane i -> p (lane i)"),
-                in_=values_grouped[c, piece][:].rearrange("p lane i t -> p (lane i t)"),
+                out=codes[:, half, some].rearrange("p lane i -> p (lane i)").bitcast(FP8X4),
+                scales=scales[:, half, some].rearrange("p lane i -> p (lane i)"),
+                in_=values_grouped[c, half, lane][:].rearrange("p lane i t -> p (lane i t)"),
             )
 
         def linear_attention(m):
@@ -256,27 +275,28 @@ def tile_flashattention_pa_t_kernel(
             c, j, half = place(m)
             if not 0 <= m < SLOTS or half != HALVES - 1:
                 return
-            hidden = work.tile([P, HALVES, P, PACK], BF16, tag="h_grp", align_bytes=64)
+            s = c * SETS + j
+            two, pos = divmod(s + 1, 2)
+            if two not in hidden_grouped:
+                hidden_grouped[two] = work.tile([P, 2, HALVES, P, PACK], BF16, tag="h_grp", align_bytes=64, name="h_grp")
             nc.vector.tensor_tensor(
-                out=hidden[:].rearrange("p half q (w e) -> p (half q) w e", e=PAIR),
+                out=hidden_grouped[two][:, pos].rearrange("p half q (w e) -> p (half q) w e", e=PAIR),
                 in0=v_sum[c, j][:].rearrange("p half q (w e) -> p (half q) w e", e=PAIR),
                 in1=gate_T[c, j][:].bitcast(BF16).rearrange("p w half (q e) -> p (half q) w e", e=PAIR),
                 op=ALU.mult,
             )
-            hidden_grouped[c, j] = hidden
 
-        def quantise_hidden(m):
-            c, j, half = place(m)
-            if not 0 <= m < SLOTS or half != HALVES - 1:
-                return
-            codes = work.tile([P, HALVES, P], U32, tag="h_codes", align_bytes=64)
-            scales = work.tile([P, HALVES, P], U8, tag="h_scales", align_bytes=64)
+        def quantise_hidden(two):
+            first = 1 if two == 0 else 0
+            last = 1 if two == CHUNKS * SETS // 2 else 2
+            codes = work.tile([P, 2, HALVES, P], U32, tag="h_codes", align_bytes=64)
+            scales = work.tile([P, 2, HALVES, P], U8, tag="h_scales", align_bytes=64)
             nc.vector.quantize_mx(
-                out=codes[:].rearrange("p half q -> p (half q)").bitcast(FP8X4),
-                scales=scales[:].rearrange("p half q -> p (half q)"),
-                in_=hidden_grouped[c, j][:].rearrange("p half q t -> p (half q t)"),
+                out=codes[:, first:last].rearrange("p s half q -> p (s half q)").bitcast(FP8X4),
+                scales=scales[:, first:last].rearrange("p s half q -> p (s half q)"),
+                in_=hidden_grouped[two][:, first:last].rearrange("p s half q t -> p (s half q t)"),
             )
-            hidden_mx[c, j] = (codes, scales)
+            hidden_mx[two] = (codes, scales)
 
         def out_rows(c, j):
             b, g = divmod(c, G)
@@ -286,36 +306,35 @@ def tile_flashattention_pa_t_kernel(
             c, j, half = place(m)
             if not 0 <= m < SLOTS or half != HALVES - 1:
                 return
-            codes, scales = hidden_mx[c, j]
+            two, pos = divmod(c * SETS + j + 1, 2)
+            codes, scales = hidden_mx[two]
             out_ps = psum.tile([P, D], F32, tag="misc")
             for k_half in range(HALVES):
                 nc.tensor.matmul_mx(
                     out=out_ps[:],
-                    lhsT=codes[:, k_half, :].bitcast(FP8X4),
-                    lhsT_scale=scales[:, k_half, :],
+                    lhsT=codes[:, pos, k_half, :].bitcast(FP8X4),
+                    lhsT_scale=scales[:, pos, k_half, :],
                     rhs=w_codes[:, k_half, :].bitcast(FP8X4),
                     rhs_scale=w_scales[:, k_half, :],
                     start=(k_half == 0),
                     stop=(k_half == HALVES - 1),
                 )
-            result = work.tile([P, D], F32, tag="result", bufs=32)
             if j % 2 == 1:
+                result = work.tile([P, D], F32, tag="result", bufs=32)
                 nc.vector.tensor_tensor(out=result[:], in0=out_ps[:], in1=bod_rows[:], op=ALU.add)
                 nc.sync.dma_start(out=out_rows(c, j), in_=result[:])
             else:
-                product = work.tile([P, D], F32, tag="product", bufs=16)
+                product = work.tile([P, D], F32, tag="product", bufs=PRODUCT_BUFS)
                 nc.scalar.copy(out=product[:], in_=out_ps[:])
-                projected[c, j] = (result, product)
+                products[c, j] = product
 
         def add_bias_and_store(m):
             c, j, half = place(m)
-            if not 0 <= m < SLOTS or half != HALVES - 1:
+            if not 0 <= m < SLOTS:
                 return
-            part = j % 2
-            result, product = projected[c, j - part]
-            cols = slice(part * (D // 2), (part + 1) * (D // 2))
-            nc.gpsimd.tensor_tensor(out=result[:, cols], in0=product[:, cols], in1=bod_rows[:, cols], op=ALU.add)
-            nc.sync.dma_start(out=out_rows(c, j - part)[:, cols], in_=result[:, cols])
+            result = work.tile([P, D], F32, tag="result", bufs=32)
+            nc.gpsimd.tensor_tensor(out=result[:], in0=products[c, j][:], in1=bod_rows[:], op=ALU.add)
+            nc.sync.dma_start(out=out_rows(c, j), in_=result[:])
 
         ident_bf = const.tile([P, P], BF16)
         masks.make_identity(nc, ident_bf[:])
@@ -330,10 +349,11 @@ def tile_flashattention_pa_t_kernel(
         load_tokens(0)
         load_values(0)
         kv_in = const.tile([P, B, E], BF16)
-        nc.sync.dma_start(out=kv_in[:], in_=kv.rearrange("b s e -> s b e"))
+        nc.sync.dma_start(out=kv_in[:, 0], in_=kv[0])
+        load_gate(0)
         load_tokens(1)
         load_values(1)
-        load_gate(0)
+        nc.sync.dma_start(out=kv_in[:, 1], in_=kv[1])
 
         w_codes = const.tile([P, HALVES, D], U32, align_bytes=64)
         nc.sync.dma_start(
@@ -352,34 +372,72 @@ def tile_flashattention_pa_t_kernel(
         load_values(2)
 
         kv_sorted = const.tile([P, B, HALVES, PACK, P], BF16)
-        for b in range(B):
-            nc.gpsimd.tensor_scalar(
-                out=kv_sorted[:, b],
-                in0=kv_in[:, b, :].rearrange("s (half i lane) -> s half lane i", half=HALVES, lane=PACK),
-                scalar1=1.0,
-                scalar2=0.0,
-                op0=ALU.mult,
-                op1=ALU.add,
-            )
 
-        for n in range(-TOKENS_LEAD, SLOTS + STORE_LAG):
-            if n >= 0 and n % SLOTS_PER_CHUNK == 0:
+        def sort_kv(b, half):
+            rows = kv_in[:, b, half * K_PASS : (half + 1) * K_PASS].rearrange("s (i lane) -> s lane i", lane=PACK)
+            nc.scalar.copy(out=kv_sorted[:, b, half], in_=rows)
+
+        transpose_tokens(0)
+        for t in range(PACK):
+            score_relu(0, t)
+        regroup_values(0, 0, 0, 2, FIRST_REGROUP[0])
+        regroup_values(0, 0, 2, 2, FIRST_REGROUP[1])
+        quantise_values(0, 0, 0, 2)
+        score_square(0, 0)
+        score_square(0, 1)
+        quantise_scores(0, 0)
+        quantise_values(0, 0, 2, 2)
+        sort_kv(0, 0)
+        sort_kv(0, 1)
+        regroup_values(0, 1, 0, 2, FIRST_REGROUP[2])
+        quantise_values(0, 1, 0, 2)
+        score_square(0, 2)
+        score_square(0, 3)
+        regroup_values(0, 1, 2, 2, FIRST_REGROUP[3])
+        quantise_scores(0, 1)
+        quantise_values(0, 1, 2, 2)
+        regroup_values(1, 0)
+        linear_attention(0)
+        linear_attention(1)
+
+        for n in range(0, SLOTS + PROJECT_LAG):
+            if n % SLOTS_PER_CHUNK == 0:
                 c = n // SLOTS_PER_CHUNK
+                if c == 2:
+                    sort_kv(1, 0)
+                    sort_kv(1, 1)
                 load_gate(c + 1)
                 load_tokens(c + 3)
                 load_values(c + 3)
             quadratic_attention(n)
             gate(n - GATE_LAG)
+            if n == SLOTS:
+                quantise_hidden(SLOTS // PERIOD)
             project(n - PROJECT_LAG)
-            if (n + LIN_LEAD) % HALVES == 0:
-                linear_attention(n + LIN_LEAD)
+            lin_slot = n + LIN_LEAD if n > 0 else HALVES
+            if lin_slot % HALVES == 0:
+                linear_attention(lin_slot)
             transpose_gate(n - GATE_T_LAG)
-            transpose_tokens(n + TOKENS_LEAD)
-            if (n + LIN_LEAD) % HALVES == 0:
-                linear_attention(n + LIN_LEAD + 1)
-            scores(n + PREPARE_LEAD)
-            quantise_hidden(n - QUANT_HIDDEN_LAG)
-            quantise_values(n + QUANT_VALUES_LEAD)
-            quantise_scores(n + QUANT_SCORES_LEAD)
-            regroup_values(n + REGROUP_LEAD)
-            add_bias_and_store(n - STORE_LAG)
+            if n == 1:
+                transpose_tokens(1)
+            if (n + TOKENS_LEAD) % SLOTS_PER_CHUNK == 0 and n + TOKENS_LEAD >= 2 * SLOTS_PER_CHUNK:
+                transpose_tokens((n + TOKENS_LEAD) // SLOTS_PER_CHUNK)
+            if lin_slot % HALVES == 0:
+                linear_attention(lin_slot + 1)
+            for piece in {1: (0, 1), 2: (2, 3), 3: (4, 5), 4: (6,), 5: (7,)}.get(n, ()):
+                scores(SLOTS_PER_CHUNK + piece)
+            if n + PREPARE_LEAD >= 2 * SLOTS_PER_CHUNK:
+                scores(n + PREPARE_LEAD)
+            if n % PERIOD == PERIOD - 1 and n < SLOTS:
+                period = n // PERIOD
+                c, half = divmod(period + 2, HALVES)
+                quantise_hidden(period)
+                if c > 1:
+                    quantise_scores(c, half)
+                elif half == 1:
+                    quantise_scores(c, 0)
+                    quantise_scores(c, 1)
+                quantise_values(c, half)
+                regroup_values((period + 3) // HALVES, (period + 3) % HALVES)
+            if n % PERIOD == PERIOD - 1 and n > PERIOD:
+                add_bias_and_store(n - PROJECT_LAG - 1)

@@ -30,8 +30,9 @@ RELU_BUFS = 2
 PRODUCT_BUFS = 4
 FIRST_SQUARES_ON_VECTOR = (1, 3)
 TOKENS_LEAD = 13
-PREPARE_LEAD = 11
+PREPARE_LEAD = 12
 LIN_LEAD = 3
+QUAD_LEAD = 1
 GATE_T_LAG = 1
 GATE_LAG = 1
 PROJECT_LAG = 5
@@ -59,6 +60,7 @@ def tile_flashattention_pa_t_kernel(
         keys_queries_T, lin_queries_T = {}, {}
         relu_scores, scores_grouped, scores_mx = {}, {}, {}
         values_grouped, values_mx = {}, {}
+        quads = {}
         gate_T, v_sum, hidden_grouped, hidden_mx, products = {}, {}, {}, {}, {}
 
         def load_tokens(c):
@@ -99,7 +101,7 @@ def tile_flashattention_pa_t_kernel(
             kq = work.tile([P, 2 * SETS, P], BF16, tag="kqT")
             if c == 0:
                 for i in range(2):
-                    part_ps = psum.tile([P, SETS, P], BF16, tag="misc")
+                    part_ps = psum.tile([P, SETS, P], BF16, tag="act", bufs=3)
                     for j in range(SETS):
                         nc.tensor.transpose(part_ps[:, j, :], tok[:, i, j, :], ident_bf[:])
                     part = kq[:, i * SETS : (i + 1) * SETS, :]
@@ -108,13 +110,13 @@ def tile_flashattention_pa_t_kernel(
                     else:
                         nc.vector.tensor_copy(out=part, in_=part_ps[:])
             else:
-                kq_ps = psum.tile([P, 2 * SETS, P], BF16, tag="misc")
+                kq_ps = psum.tile([P, 2 * SETS, P], BF16, tag="act", bufs=3)
                 for i in range(2):
                     for j in range(SETS):
                         nc.tensor.transpose(kq_ps[:, i * SETS + j, :], tok[:, i, j, :], ident_bf[:])
                 nc.scalar.copy(out=kq[:], in_=kq_ps[:])
             keys_queries_T[c] = kq
-            lin_ps = psum.tile([P, SETS, P], BF16, tag="misc")
+            lin_ps = psum.tile([P, SETS, P], BF16, tag="act", bufs=3)
             for j in range(SETS):
                 nc.tensor.transpose(lin_ps[:, j, :], tok[:, 2, j, :], ident_bf[:])
             lin = work.tile([P, SETS, P], BF16, tag="linT", bufs=3)
@@ -125,7 +127,7 @@ def tile_flashattention_pa_t_kernel(
             if t == 0:
                 relu_scores[c] = work.tile([P, PACK, C], F32, tag="relu", bufs=RELU_BUFS, name="relu")
             kq = keys_queries_T[c]
-            qk_ps = psum.tile([P, C], F32, tag="misc")
+            qk_ps = psum.tile([P, C], F32, tag="act", bufs=3)
             nc.tensor.matmul(
                 out=qk_ps[:],
                 lhsT=kq[:, t, :],
@@ -220,7 +222,7 @@ def tile_flashattention_pa_t_kernel(
             c, j, half = place(m)
             if not 0 <= m < SLOTS:
                 return
-            lin_ps = psum.tile([P, PACK, P], F32, tag="v_lin")
+            lin_ps = psum.tile([P, PACK, P], F32, tag="act", bufs=3)
             for lane in range(PACK):
                 nc.tensor.matmul(
                     out=lin_ps[:, lane, :],
@@ -240,7 +242,8 @@ def tile_flashattention_pa_t_kernel(
             v_codes, v_scales = values_mx[c]
             a_codes, a_scales = scores_mx[c]
             cols = slice(j * P, (j + 1) * P)
-            quad_ps = psum.tile([P, PACK, P], F32, tag="v_quad")
+            quad_ps = psum.tile([P, PACK, P], F32, tag="vec", bufs=3)
+            quads[m] = quad_ps
             for lane in range(PACK):
                 nc.tensor.matmul_mx(
                     out=quad_ps[:, lane, :],
@@ -251,6 +254,12 @@ def tile_flashattention_pa_t_kernel(
                     start=True,
                     stop=True,
                 )
+
+        def add_quadratic(m):
+            c, j, half = place(m)
+            if not 0 <= m < SLOTS:
+                return
+            quad_ps = quads[m]
             nc.vector.tensor_tensor(
                 out=v_sum[c, j][:, half],
                 in0=v_sum[c, j][:, half],
@@ -308,7 +317,8 @@ def tile_flashattention_pa_t_kernel(
                 return
             two, pos = divmod(c * SETS + j + 1, 2)
             codes, scales = hidden_mx[two]
-            out_ps = psum.tile([P, D], F32, tag="misc")
+            ring, banks = ("vec", 3) if j % 2 == 1 else ("act", 3)
+            out_ps = psum.tile([P, D], F32, tag=ring, bufs=banks, name="out_ps")
             for k_half in range(HALVES):
                 nc.tensor.matmul_mx(
                     out=out_ps[:],
@@ -400,6 +410,8 @@ def tile_flashattention_pa_t_kernel(
         linear_attention(0)
         linear_attention(1)
 
+        for m in range(QUAD_LEAD):
+            quadratic_attention(m)
         for n in range(0, SLOTS + PROJECT_LAG):
             if n % SLOTS_PER_CHUNK == 0:
                 c = n // SLOTS_PER_CHUNK
@@ -409,7 +421,8 @@ def tile_flashattention_pa_t_kernel(
                 load_gate(c + 1)
                 load_tokens(c + 3)
                 load_values(c + 3)
-            quadratic_attention(n)
+            quadratic_attention(n + QUAD_LEAD)
+            add_quadratic(n)
             gate(n - GATE_LAG)
             if n == SLOTS:
                 quantise_hidden(SLOTS // PERIOD)
@@ -428,15 +441,14 @@ def tile_flashattention_pa_t_kernel(
                 scores(SLOTS_PER_CHUNK + piece)
             if n + PREPARE_LEAD >= 2 * SLOTS_PER_CHUNK:
                 scores(n + PREPARE_LEAD)
+            if n == 6:
+                quantise_scores(1, 0)
             if n % PERIOD == PERIOD - 1 and n < SLOTS:
                 period = n // PERIOD
                 c, half = divmod(period + 2, HALVES)
                 quantise_hidden(period)
-                if c > 1:
+                if (c, half) != (1, 0):
                     quantise_scores(c, half)
-                elif half == 1:
-                    quantise_scores(c, 0)
-                    quantise_scores(c, 1)
                 quantise_values(c, half)
                 regroup_values((period + 3) // HALVES, (period + 3) % HALVES)
             if n % PERIOD == PERIOD - 1 and n > PERIOD:

@@ -26,10 +26,12 @@ FLOPS = 2 * CHUNKS * (C * C * S + C * C * E + C * S * E + C * E * D)
 SLOTS_PER_CHUNK = SETS * HALVES
 SLOTS = CHUNKS * SLOTS_PER_CHUNK
 PERIOD = 4
+LAST_GP = 27
 RELU_BUFS = 2
-PRODUCT_BUFS = 4
+PRODUCT_BUFS = 6
+RESULT_BUFS = 12
 FIRST_SQUARES_ON_VECTOR = (1, 3)
-TOKENS_LEAD = 13
+TOKENS_LEAD = 14
 PREPARE_LEAD = 12
 LIN_LEAD = 3
 QUAD_LEAD = 1
@@ -317,34 +319,46 @@ def tile_flashattention_pa_t_kernel(
                 return
             two, pos = divmod(c * SETS + j + 1, 2)
             codes, scales = hidden_mx[two]
-            ring, banks = ("vec", 3) if j % 2 == 1 else ("act", 3)
-            out_ps = psum.tile([P, D], F32, tag=ring, bufs=banks, name="out_ps")
-            for k_half in range(HALVES):
-                nc.tensor.matmul_mx(
-                    out=out_ps[:],
-                    lhsT=codes[:, pos, k_half, :].bitcast(FP8X4),
-                    lhsT_scale=scales[:, pos, k_half, :],
-                    rhs=w_codes[:, k_half, :].bitcast(FP8X4),
-                    rhs_scale=w_scales[:, k_half, :],
-                    start=(k_half == 0),
-                    stop=(k_half == HALVES - 1),
-                )
-            if j % 2 == 1:
-                result = work.tile([P, D], F32, tag="result", bufs=32)
-                nc.vector.tensor_tensor(out=result[:], in0=out_ps[:], in1=bod_rows[:], op=ALU.add)
-                nc.sync.dma_start(out=out_rows(c, j), in_=result[:])
-            else:
+            def product_columns(cols, ring):
+                out_ps = psum.tile([P, cols.stop - cols.start], F32, tag=ring, bufs=3, name="out_ps")
+                for k_half in range(HALVES):
+                    nc.tensor.matmul_mx(
+                        out=out_ps[:],
+                        lhsT=codes[:, pos, k_half, :].bitcast(FP8X4),
+                        lhsT_scale=scales[:, pos, k_half, :],
+                        rhs=w_codes[:, k_half, cols].bitcast(FP8X4),
+                        rhs_scale=w_scales[:, k_half, cols],
+                        start=(k_half == 0),
+                        stop=(k_half == HALVES - 1),
+                    )
+                return out_ps
+
+            for_gpsimd = slice(0, gpsimd_columns(c, j))
+            if for_gpsimd.stop > 0:
+                out_ps = product_columns(for_gpsimd, "act")
                 product = work.tile([P, D], F32, tag="product", bufs=PRODUCT_BUFS)
-                nc.scalar.copy(out=product[:], in_=out_ps[:])
+                nc.scalar.copy(out=product[:, for_gpsimd], in_=out_ps[:])
                 products[c, j] = product
+            rest = slice(for_gpsimd.stop, D)
+            if rest.start < D:
+                out_ps = product_columns(rest, "vec")
+                result = work.tile([P, D], F32, tag="result_v", bufs=RESULT_BUFS)
+                nc.vector.tensor_tensor(out=result[:, rest], in0=out_ps[:], in1=bod_rows[:, rest], op=ALU.add)
+                nc.sync.dma_start(out=out_rows(c, j)[:, rest], in_=result[:, rest])
+
+        def gpsimd_columns(c, j):
+            if c * SETS + j > LAST_GP:
+                return 0
+            return (D, 256)[j % 2]
 
         def add_bias_and_store(m):
             c, j, half = place(m)
-            if not 0 <= m < SLOTS:
+            if not 0 <= m < SLOTS or gpsimd_columns(c, j) == 0:
                 return
-            result = work.tile([P, D], F32, tag="result", bufs=32)
-            nc.gpsimd.tensor_tensor(out=result[:], in0=products[c, j][:], in1=bod_rows[:], op=ALU.add)
-            nc.sync.dma_start(out=out_rows(c, j), in_=result[:])
+            cols = slice(0, gpsimd_columns(c, j))
+            result = work.tile([P, D], F32, tag="result_g", bufs=RESULT_BUFS)
+            nc.gpsimd.tensor_tensor(out=result[:, cols], in0=products[c, j][:, cols], in1=bod_rows[:, cols], op=ALU.add)
+            nc.sync.dma_start(out=out_rows(c, j)[:, cols], in_=result[:, cols])
 
         ident_bf = const.tile([P, P], BF16)
         masks.make_identity(nc, ident_bf[:])
@@ -357,9 +371,9 @@ def tile_flashattention_pa_t_kernel(
         nc.vector.tensor_copy(out=key_bias[:], in_=bias_bf[:])
 
         load_tokens(0)
-        load_values(0)
         kv_in = const.tile([P, B, E], BF16)
         nc.sync.dma_start(out=kv_in[:, 0], in_=kv[0])
+        load_values(0)
         load_gate(0)
         load_tokens(1)
         load_values(1)
@@ -385,8 +399,15 @@ def tile_flashattention_pa_t_kernel(
 
         def sort_kv(b, half):
             rows = kv_in[:, b, half * K_PASS : (half + 1) * K_PASS].rearrange("s (i lane) -> s lane i", lane=PACK)
-            nc.scalar.copy(out=kv_sorted[:, b, half], in_=rows)
+            if b == 0:
+                nc.gpsimd.tensor_scalar(
+                    out=kv_sorted[:, b, half], in0=rows, scalar1=1.0, scalar2=0.0, op0=ALU.mult, op1=ALU.add
+                )
+            else:
+                nc.scalar.copy(out=kv_sorted[:, b, half], in_=rows)
 
+        sort_kv(0, 0)
+        sort_kv(0, 1)
         transpose_tokens(0)
         for t in range(PACK):
             score_relu(0, t)
@@ -397,8 +418,6 @@ def tile_flashattention_pa_t_kernel(
         score_square(0, 1)
         quantise_scores(0, 0)
         quantise_values(0, 0, 2, 2)
-        sort_kv(0, 0)
-        sort_kv(0, 1)
         regroup_values(0, 1, 0, 2, FIRST_REGROUP[2])
         quantise_values(0, 1, 0, 2)
         score_square(0, 2)
@@ -409,9 +428,12 @@ def tile_flashattention_pa_t_kernel(
         regroup_values(1, 0)
         linear_attention(0)
         linear_attention(1)
+        transpose_tokens(1)
 
         for m in range(QUAD_LEAD):
             quadratic_attention(m)
+        for t in range(4):
+            score_relu(1, t)
         for n in range(0, SLOTS + PROJECT_LAG):
             if n % SLOTS_PER_CHUNK == 0:
                 c = n // SLOTS_PER_CHUNK
@@ -431,17 +453,15 @@ def tile_flashattention_pa_t_kernel(
             if lin_slot % HALVES == 0:
                 linear_attention(lin_slot)
             transpose_gate(n - GATE_T_LAG)
-            if n == 1:
-                transpose_tokens(1)
             if (n + TOKENS_LEAD) % SLOTS_PER_CHUNK == 0 and n + TOKENS_LEAD >= 2 * SLOTS_PER_CHUNK:
                 transpose_tokens((n + TOKENS_LEAD) // SLOTS_PER_CHUNK)
             if lin_slot % HALVES == 0:
                 linear_attention(lin_slot + 1)
-            for piece in {1: (0, 1), 2: (2, 3), 3: (4, 5), 4: (6,), 5: (7,)}.get(n, ()):
+            for piece in {0: (4,), 1: (5,), 2: (6,), 3: (7,)}.get(n, ()):
                 scores(SLOTS_PER_CHUNK + piece)
             if n + PREPARE_LEAD >= 2 * SLOTS_PER_CHUNK:
                 scores(n + PREPARE_LEAD)
-            if n == 6:
+            if n == 5:
                 quantise_scores(1, 0)
             if n % PERIOD == PERIOD - 1 and n < SLOTS:
                 period = n // PERIOD
@@ -452,4 +472,5 @@ def tile_flashattention_pa_t_kernel(
                 quantise_values(c, half)
                 regroup_values((period + 3) // HALVES, (period + 3) % HALVES)
             if n % PERIOD == PERIOD - 1 and n > PERIOD:
+                add_bias_and_store(n - PROJECT_LAG - 3)
                 add_bias_and_store(n - PROJECT_LAG - 1)

@@ -356,7 +356,10 @@ def tile_flashattention_pa_t_kernel(
             if not 0 <= m < SLOTS or gpsimd_columns(c, j) == 0:
                 return
             cols = slice(0, gpsimd_columns(c, j))
-            result = work.tile([P, D], F32, tag="result_g", bufs=RESULT_BUFS)
+            if m == SLOTS - 2 * PERIOD - 1 - (PROJECT_LAG + 3):
+                result = work.tile([P, D], F32, tag="v_grp", bufs=1, align_bytes=64)
+            else:
+                result = work.tile([P, D], F32, tag="result_g", bufs=RESULT_BUFS)
             nc.gpsimd.tensor_tensor(out=result[:, cols], in0=products[c, j][:, cols], in1=bod_rows[:, cols], op=ALU.add)
             nc.sync.dma_start(out=out_rows(c, j)[:, cols], in_=result[:, cols])
 
@@ -364,6 +367,12 @@ def tile_flashattention_pa_t_kernel(
         masks.make_identity(nc, ident_bf[:])
         ident_f32 = const.tile([P, P], F32)
         masks.make_identity(nc, ident_f32[:])
+
+        zeros = const.tile([P, P], BF16)
+        nc.vector.memset(zeros[:], 0.0)
+        warm_ps = psum.tile([P, P], F32, tag="act", bufs=3)
+        for i in range(10):
+            nc.tensor.matmul(out=warm_ps[:], lhsT=zeros[:], rhs=zeros[:], start=True, stop=True)
 
         bias_bf = const.tile([P, PACK], BF16)
         nc.sync.dma_start(out=bias_bf[:], in_=rel_bias.rearrange("(p t) -> p t", t=PACK))
@@ -374,10 +383,10 @@ def tile_flashattention_pa_t_kernel(
         kv_in = const.tile([P, B, E], BF16)
         nc.sync.dma_start(out=kv_in[:, 0], in_=kv[0])
         load_values(0)
-        load_gate(0)
         load_tokens(1)
+        load_gate(0)
         load_values(1)
-        nc.sync.dma_start(out=kv_in[:, 1], in_=kv[1])
+        load_tokens(2)
 
         w_codes = const.tile([P, HALVES, D], U32, align_bytes=64)
         nc.sync.dma_start(
@@ -390,10 +399,10 @@ def tile_flashattention_pa_t_kernel(
                 out=w_scales[32 * quadrant : 32 * quadrant + 4].bitcast(I32),
                 in_=Wod_scales[:, 4 * quadrant : 4 * quadrant + 4, :].rearrange("half r n -> r half n").bitcast(I32),
             )
+        load_values(2)
+        nc.sync.dma_start(out=kv_in[:, 1], in_=kv[1])
         bod_rows = const.tile([P, D], BF16)
         nc.sync.dma_start(out=bod_rows[:], in_=bod.partition_broadcast(P))
-        load_tokens(2)
-        load_values(2)
 
         kv_sorted = const.tile([P, B, HALVES, PACK, P], BF16)
 
@@ -413,15 +422,15 @@ def tile_flashattention_pa_t_kernel(
             score_relu(0, t)
         regroup_values(0, 0, 0, 2, FIRST_REGROUP[0])
         regroup_values(0, 0, 2, 2, FIRST_REGROUP[1])
-        quantise_values(0, 0, 0, 2)
         score_square(0, 0)
         score_square(0, 1)
+        quantise_values(0, 0, 0, 2)
         quantise_scores(0, 0)
         quantise_values(0, 0, 2, 2)
         regroup_values(0, 1, 0, 2, FIRST_REGROUP[2])
-        quantise_values(0, 1, 0, 2)
         score_square(0, 2)
         score_square(0, 3)
+        quantise_values(0, 1, 0, 2)
         regroup_values(0, 1, 2, 2, FIRST_REGROUP[3])
         quantise_scores(0, 1)
         quantise_values(0, 1, 2, 2)
@@ -437,12 +446,13 @@ def tile_flashattention_pa_t_kernel(
         for n in range(0, SLOTS + PROJECT_LAG):
             if n % SLOTS_PER_CHUNK == 0:
                 c = n // SLOTS_PER_CHUNK
-                if c == 2:
-                    sort_kv(1, 0)
-                    sort_kv(1, 1)
                 load_gate(c + 1)
                 load_tokens(c + 3)
                 load_values(c + 3)
+            if n == 19:
+                sort_kv(1, 0)
+            if n == 23:
+                sort_kv(1, 1)
             quadratic_attention(n + QUAD_LEAD)
             add_quadratic(n)
             gate(n - GATE_LAG)
@@ -461,14 +471,11 @@ def tile_flashattention_pa_t_kernel(
                 scores(SLOTS_PER_CHUNK + piece)
             if n + PREPARE_LEAD >= 2 * SLOTS_PER_CHUNK:
                 scores(n + PREPARE_LEAD)
-            if n == 5:
-                quantise_scores(1, 0)
             if n % PERIOD == PERIOD - 1 and n < SLOTS:
                 period = n // PERIOD
                 c, half = divmod(period + 2, HALVES)
                 quantise_hidden(period)
-                if (c, half) != (1, 0):
-                    quantise_scores(c, half)
+                quantise_scores(c, half)
                 quantise_values(c, half)
                 regroup_values((period + 3) // HALVES, (period + 3) % HALVES)
             if n % PERIOD == PERIOD - 1 and n > PERIOD:

from contextlib import ExitStack

import concourse.masks as masks
import concourse.mybir as mybir

BF16 = mybir.dt.bfloat16
F32 = mybir.dt.float32
I32 = mybir.dt.int32
U32 = mybir.dt.uint32
U8 = mybir.dt.uint8
FP8X4 = mybir.dt.float8_e4m3fn_x4
ACT = mybir.ActivationFunctionType
ALU = mybir.AluOpType

B, G, C, S, E, D = 2, 4, 512, 128, 1024, 512
CHUNKS = B * G
P = 128
PACK = 4
K_PASS = P * PACK
SETS = C // P
HALVES = E // K_PASS
PAIR = 2

FLOPS = 2 * CHUNKS * (C * C * S + C * C * E + C * S * E + C * E * D)

SLOTS_PER_CHUNK = SETS * HALVES
SLOTS = CHUNKS * SLOTS_PER_CHUNK
PERIOD = 4
LAST_GP = 27
RELU_BUFS = 2
PRODUCT_BUFS = 6
RESULT_BUFS = 12
FIRST_SQUARES_ON_VECTOR = (1, 3)
TOKENS_LEAD = 14
PREPARE_LEAD = 12
LIN_LEAD = 3
QUAD_LEAD = 1
GATE_T_LAG = 1
GATE_LAG = 1
PROJECT_LAG = 5
FIRST_REGROUP = ("vector", "scalar", "vector", "vector")


def place(m):
    c, piece = divmod(m, SLOTS_PER_CHUNK)
    j, half = divmod(piece, HALVES)
    return c, j, half


def tile_flashattention_pa_t_kernel(
    tc, q_quad, k_quad, q_lin, kv, v, u, rel_bias, Wod_words, Wod_scales, bod, out
):
    nc = tc.nc
    with ExitStack() as pools:
        const = pools.enter_context(tc.tile_pool(name="const", bufs=1))
        loads = pools.enter_context(tc.tile_pool(name="loads", bufs=3))
        work = pools.enter_context(tc.tile_pool(name="work", bufs=2))
        psum = pools.enter_context(tc.psum_pool(name="psum", bufs=2))
        pools.enter_context(tc.manual_schedule())

        tokens_in, values_in, gate_in = {}, {}, {}
        keys_queries_T, lin_queries_T = {}, {}
        relu_scores, scores_grouped, scores_mx = {}, {}, {}
        values_grouped, values_mx = {}, {}
        quads = {}
        gate_T, v_sum, hidden_grouped, hidden_mx, products = {}, {}, {}, {}, {}

        def load_tokens(c):
            if c >= CHUNKS:
                return
            b, g = divmod(c, G)
            tok = loads.tile([P, 3, SETS, S], BF16, tag="tokens")
            for i, src in enumerate((k_quad, q_quad, q_lin)):
                nc.sync.dma_start(out=tok[:, i], in_=src[b, g].rearrange("(p j) s -> p j s", j=SETS))
            tokens_in[c] = tok

        def load_values(c):
            if c >= CHUNKS:
                return
            b, g = divmod(c, G)
            val = loads.tile([P, PACK, E], BF16, tag="values")
            rows = v[b, g].rearrange("(p t) e -> p t e", t=PACK)
            if c == 0:
                for half in range(HALVES):
                    cols = slice(half * K_PASS, (half + 1) * K_PASS)
                    nc.sync.dma_start(out=val[:, :, cols], in_=rows[:, :, cols])
            else:
                nc.sync.dma_start(out=val[:], in_=rows)
            values_in[c] = val

        def load_gate(c):
            if c >= CHUNKS:
                return
            b, g = divmod(c, G)
            gat = loads.tile([P, SETS, E], BF16, tag="gate")
            nc.sync.dma_start(out=gat[:], in_=u[b, g].rearrange("(p j) e -> p j e", j=SETS))
            gate_in[c] = gat

        def transpose_tokens(c):
            if not 0 <= c < CHUNKS:
                return
            tok = tokens_in[c]
            kq = work.tile([P, 2 * SETS, P], BF16, tag="kqT")
            if c == 0:
                for i in range(2):
                    part_ps = psum.tile([P, SETS, P], BF16, tag="act", bufs=3)
                    for j in range(SETS):
                        nc.tensor.transpose(part_ps[:, j, :], tok[:, i, j, :], ident_bf[:])
                    part = kq[:, i * SETS : (i + 1) * SETS, :]
                    if i == 0:
                        nc.scalar.copy(out=part, in_=part_ps[:])
                    else:
                        nc.vector.tensor_copy(out=part, in_=part_ps[:])
            else:
                kq_ps = psum.tile([P, 2 * SETS, P], BF16, tag="act", bufs=3)
                for i in range(2):
                    for j in range(SETS):
                        nc.tensor.transpose(kq_ps[:, i * SETS + j, :], tok[:, i, j, :], ident_bf[:])
                nc.scalar.copy(out=kq[:], in_=kq_ps[:])
            keys_queries_T[c] = kq
            lin_ps = psum.tile([P, SETS, P], BF16, tag="act", bufs=3)
            for j in range(SETS):
                nc.tensor.transpose(lin_ps[:, j, :], tok[:, 2, j, :], ident_bf[:])
            lin = work.tile([P, SETS, P], BF16, tag="linT", bufs=3)
            nc.scalar.copy(out=lin[:], in_=lin_ps[:])
            lin_queries_T[c] = lin

        def score_relu(c, t):
            if t == 0:
                relu_scores[c] = work.tile([P, PACK, C], F32, tag="relu", bufs=RELU_BUFS, name="relu")
            kq = keys_queries_T[c]
            qk_ps = psum.tile([P, C], F32, tag="act", bufs=3)
            nc.tensor.matmul(
                out=qk_ps[:],
                lhsT=kq[:, t, :],
                rhs=kq[:, SETS : 2 * SETS, :].rearrange("s j p -> s (j p)"),
                start=True,
                stop=True,
            )
            if c == 0 and t % 2 == 1:
                nc.vector.tensor_scalar(
                    out=relu_scores[c][:, t, :],
                    in0=qk_ps[:],
                    scalar1=key_bias[:, t : t + 1],
                    scalar2=0.0,
                    op0=ALU.add,
                    op1=ALU.max,
                )
            else:
                nc.scalar.activation(
                    out=relu_scores[c][:, t, :], in_=qk_ps[:], func=ACT.Relu, bias=key_bias[:, t : t + 1], scale=1.0
                )

        def score_square(c, j):
            if j == 0:
                scores_grouped[c] = work.tile([P, C, PACK], BF16, tag="a_grp", align_bytes=64, name="a_grp")
            cols = slice(j * P, (j + 1) * P)
            relu_grouped = relu_scores[c][:, :, cols].rearrange("p t q -> p q t")
            if c == 0 and j in FIRST_SQUARES_ON_VECTOR:
                nc.vector.tensor_tensor(
                    out=scores_grouped[c][:, cols, :], in0=relu_grouped, in1=relu_grouped, op=ALU.mult
                )
            else:
                nc.scalar.activation(out=scores_grouped[c][:, cols, :], in_=relu_grouped, func=ACT.Square)

        def scores(m):
            c, piece = divmod(m, SLOTS_PER_CHUNK)
            if not 0 <= c < CHUNKS:
                return
            if piece < PACK:
                score_relu(c, piece)
            else:
                score_square(c, piece - PACK)

        def quantise_scores(c, pair):
            if not 0 <= c < CHUNKS:
                return
            if pair == 0:
                codes = work.tile([P, C], U32, tag="a_codes", align_bytes=64)
                scales = work.tile([P, C], U8, tag="a_scales", align_bytes=64)
                scores_mx[c] = (codes, scales)
            codes, scales = scores_mx[c]
            cols = slice(pair * 2 * P, (pair + 1) * 2 * P)
            nc.vector.quantize_mx(
                out=codes[:, cols].bitcast(FP8X4),
                scales=scales[:, cols],
                in_=scores_grouped[c][:, cols].rearrange("p q t -> p (q t)"),
            )

        def regroup_values(c, half, lane=0, lanes=PACK, who="gpsimd"):
            if not 0 <= c < CHUNKS:
                return
            tag = "v_grp_scalar" if who == "scalar" else "v_grp"
            grouped = work.tile([P, lanes, P, PACK], BF16, tag=tag, bufs=1, align_bytes=64, name="v_grp")
            rows = values_in[c][:, :, half * K_PASS : (half + 1) * K_PASS].rearrange(
                "p t (i lane) -> p lane i t", lane=PACK
            )[:, lane : lane + lanes]
            if who == "gpsimd":
                nc.gpsimd.tensor_scalar(
                    out=grouped[:], in0=rows, scalar1=1.0, scalar2=0.0, op0=ALU.mult, op1=ALU.add
                )
            elif who == "scalar":
                nc.scalar.copy(out=grouped[:], in_=rows)
            else:
                nc.vector.tensor_copy(out=grouped[:], in_=rows)
            values_grouped[c, half, lane] = grouped

        def quantise_values(c, half, lane=0, lanes=PACK):
            if not 0 <= c < CHUNKS:
                return
            if half == 0 and lane == 0:
                codes = work.tile([P, HALVES, PACK, P], U32, tag="v_codes", align_bytes=64)
                scales = work.tile([P, HALVES, PACK, P], U8, tag="v_scales", align_bytes=64)
                values_mx[c] = (codes, scales)
            codes, scales = values_mx[c]
            some = slice(lane, lane + lanes)
            nc.vector.quantize_mx(
                out=codes[:, half, some].rearrange("p lane i -> p (lane i)").bitcast(FP8X4),
                scales=scales[:, half, some].rearrange("p lane i -> p (lane i)"),
                in_=values_grouped[c, half, lane][:].rearrange("p lane i t -> p (lane i t)"),
            )

        def linear_attention(m):
            c, j, half = place(m)
            if not 0 <= m < SLOTS:
                return
            lin_ps = psum.tile([P, PACK, P], F32, tag="act", bufs=3)
            for lane in range(PACK):
                nc.tensor.matmul(
                    out=lin_ps[:, lane, :],
                    lhsT=kv_sorted[:, c // G, half, lane, :],
                    rhs=lin_queries_T[c][:, j, :],
                    start=True,
                    stop=True,
                )
            if half == 0:
                v_sum[c, j] = work.tile([P, HALVES, P, PACK], F32, tag="v_sum", bufs=4, name="v_sum")
            nc.scalar.copy(out=v_sum[c, j][:, half], in_=lin_ps[:].rearrange("p lane q -> p q lane"))

        def quadratic_attention(m):
            c, j, half = place(m)
            if not 0 <= m < SLOTS:
                return
            v_codes, v_scales = values_mx[c]
            a_codes, a_scales = scores_mx[c]
            cols = slice(j * P, (j + 1) * P)
            quad_ps = psum.tile([P, PACK, P], F32, tag="vec", bufs=3)
            quads[m] = quad_ps
            for lane in range(PACK):
                nc.tensor.matmul_mx(
                    out=quad_ps[:, lane, :],
                    lhsT=v_codes[:, half, lane, :].bitcast(FP8X4),
                    lhsT_scale=v_scales[:, half, lane, :],
                    rhs=a_codes[:, cols].bitcast(FP8X4),
                    rhs_scale=a_scales[:, cols],
                    start=True,
                    stop=True,
                )

        def add_quadratic(m):
            c, j, half = place(m)
            if not 0 <= m < SLOTS:
                return
            quad_ps = quads[m]
            nc.vector.tensor_tensor(
                out=v_sum[c, j][:, half],
                in0=v_sum[c, j][:, half],
                in1=quad_ps[:].rearrange("p lane q -> p q lane"),
                op=ALU.add,
            )

        def transpose_gate(m):
            c, j, half = place(m)
            if not 0 <= m < SLOTS or half != 0:
                return
            words = gate_in[c][:, j, :].bitcast(F32)
            bank = psum.tile([P, PAIR, HALVES, P], F32, tag="gate_T")
            for k_half in range(HALVES):
                for w in range(PAIR):
                    first = k_half * (K_PASS // PAIR) + w
                    last = (k_half + 1) * (K_PASS // PAIR)
                    nc.tensor.transpose(bank[:, w, k_half, :], words[:, first:last:PAIR], ident_f32[:])
            gate_T[c, j] = bank

        def gate(m):
            c, j, half = place(m)
            if not 0 <= m < SLOTS or half != HALVES - 1:
                return
            s = c * SETS + j
            two, pos = divmod(s + 1, 2)
            if two not in hidden_grouped:
                hidden_grouped[two] = work.tile([P, 2, HALVES, P, PACK], BF16, tag="h_grp", align_bytes=64, name="h_grp")
            nc.vector.tensor_tensor(
                out=hidden_grouped[two][:, pos].rearrange("p half q (w e) -> p (half q) w e", e=PAIR),
                in0=v_sum[c, j][:].rearrange("p half q (w e) -> p (half q) w e", e=PAIR),
                in1=gate_T[c, j][:].bitcast(BF16).rearrange("p w half (q e) -> p (half q) w e", e=PAIR),
                op=ALU.mult,
            )

        def quantise_hidden(two):
            first = 1 if two == 0 else 0
            last = 1 if two == CHUNKS * SETS // 2 else 2
            codes = work.tile([P, 2, HALVES, P], U32, tag="h_codes", align_bytes=64)
            scales = work.tile([P, 2, HALVES, P], U8, tag="h_scales", align_bytes=64)
            nc.vector.quantize_mx(
                out=codes[:, first:last].rearrange("p s half q -> p (s half q)").bitcast(FP8X4),
                scales=scales[:, first:last].rearrange("p s half q -> p (s half q)"),
                in_=hidden_grouped[two][:, first:last].rearrange("p s half q t -> p (s half q t)"),
            )
            hidden_mx[two] = (codes, scales)

        def out_rows(c, j):
            b, g = divmod(c, G)
            return out[b, g].rearrange("(p j) d -> p j d", j=SETS)[:, j, :]

        def project(m):
            c, j, half = place(m)
            if not 0 <= m < SLOTS or half != HALVES - 1:
                return
            two, pos = divmod(c * SETS + j + 1, 2)
            codes, scales = hidden_mx[two]
            def product_columns(cols, ring):
                out_ps = psum.tile([P, cols.stop - cols.start], F32, tag=ring, bufs=3, name="out_ps")
                for k_half in range(HALVES):
                    nc.tensor.matmul_mx(
                        out=out_ps[:],
                        lhsT=codes[:, pos, k_half, :].bitcast(FP8X4),
                        lhsT_scale=scales[:, pos, k_half, :],
                        rhs=w_codes[:, k_half, cols].bitcast(FP8X4),
                        rhs_scale=w_scales[:, k_half, cols],
                        start=(k_half == 0),
                        stop=(k_half == HALVES - 1),
                    )
                return out_ps

            for_gpsimd = slice(0, gpsimd_columns(c, j))
            if for_gpsimd.stop > 0:
                out_ps = product_columns(for_gpsimd, "act")
                product = work.tile([P, D], F32, tag="product", bufs=PRODUCT_BUFS)
                nc.scalar.copy(out=product[:, for_gpsimd], in_=out_ps[:])
                products[c, j] = product
            rest = slice(for_gpsimd.stop, D)
            if rest.start < D:
                out_ps = product_columns(rest, "vec")
                result = work.tile([P, D], F32, tag="result_v", bufs=RESULT_BUFS)
                nc.vector.tensor_tensor(out=result[:, rest], in0=out_ps[:], in1=bod_rows[:, rest], op=ALU.add)
                nc.sync.dma_start(out=out_rows(c, j)[:, rest], in_=result[:, rest])

        def gpsimd_columns(c, j):
            if c * SETS + j > LAST_GP:
                return 0
            return (D, 256)[j % 2]

        def add_bias_and_store(m):
            c, j, half = place(m)
            if not 0 <= m < SLOTS or gpsimd_columns(c, j) == 0:
                return
            cols = slice(0, gpsimd_columns(c, j))
            if m == SLOTS - 2 * PERIOD - 1 - (PROJECT_LAG + 3):
                result = work.tile([P, D], F32, tag="v_grp", bufs=1, align_bytes=64)
            else:
                result = work.tile([P, D], F32, tag="result_g", bufs=RESULT_BUFS)
            nc.gpsimd.tensor_tensor(out=result[:, cols], in0=products[c, j][:, cols], in1=bod_rows[:, cols], op=ALU.add)
            nc.sync.dma_start(out=out_rows(c, j)[:, cols], in_=result[:, cols])

        ident_bf = const.tile([P, P], BF16)
        masks.make_identity(nc, ident_bf[:])
        ident_f32 = const.tile([P, P], F32)
        masks.make_identity(nc, ident_f32[:])

        zeros = const.tile([P, P], BF16)
        nc.vector.memset(zeros[:], 0.0)
        warm_ps = psum.tile([P, P], F32, tag="act", bufs=3)
        for i in range(10):
            nc.tensor.matmul(out=warm_ps[:], lhsT=zeros[:], rhs=zeros[:], start=True, stop=True)

        bias_bf = const.tile([P, PACK], BF16)
        nc.sync.dma_start(out=bias_bf[:], in_=rel_bias.rearrange("(p t) -> p t", t=PACK))
        key_bias = const.tile([P, PACK], F32)
        nc.vector.tensor_copy(out=key_bias[:], in_=bias_bf[:])

        load_tokens(0)
        kv_in = const.tile([P, B, E], BF16)
        nc.sync.dma_start(out=kv_in[:, 0], in_=kv[0])
        load_values(0)
        load_tokens(1)
        load_gate(0)
        load_values(1)
        load_tokens(2)

        w_codes = const.tile([P, HALVES, D], U32, align_bytes=64)
        nc.sync.dma_start(
            out=w_codes[:].bitcast(I32), in_=Wod_words.rearrange("half p n t -> p half (n t)").bitcast(I32)
        )
        w_scales = const.tile([P, HALVES, D], U8, align_bytes=64)
        nc.vector.memset(w_scales[:].bitcast(I32), 0)
        for quadrant in range(4):
            nc.sync.dma_start(
                out=w_scales[32 * quadrant : 32 * quadrant + 4].bitcast(I32),
                in_=Wod_scales[:, 4 * quadrant : 4 * quadrant + 4, :].rearrange("half r n -> r half n").bitcast(I32),
            )
        load_values(2)
        nc.sync.dma_start(out=kv_in[:, 1], in_=kv[1])
        bod_rows = const.tile([P, D], BF16)
        nc.sync.dma_start(out=bod_rows[:], in_=bod.partition_broadcast(P))

        kv_sorted = const.tile([P, B, HALVES, PACK, P], BF16)

        def sort_kv(b, half):
            rows = kv_in[:, b, half * K_PASS : (half + 1) * K_PASS].rearrange("s (i lane) -> s lane i", lane=PACK)
            if b == 0:
                nc.gpsimd.tensor_scalar(
                    out=kv_sorted[:, b, half], in0=rows, scalar1=1.0, scalar2=0.0, op0=ALU.mult, op1=ALU.add
                )
            else:
                nc.scalar.copy(out=kv_sorted[:, b, half], in_=rows)

        sort_kv(0, 0)
        sort_kv(0, 1)
        transpose_tokens(0)
        for t in range(PACK):
            score_relu(0, t)
        regroup_values(0, 0, 0, 2, FIRST_REGROUP[0])
        regroup_values(0, 0, 2, 2, FIRST_REGROUP[1])
        score_square(0, 0)
        score_square(0, 1)
        quantise_values(0, 0, 0, 2)
        quantise_scores(0, 0)
        quantise_values(0, 0, 2, 2)
        regroup_values(0, 1, 0, 2, FIRST_REGROUP[2])
        score_square(0, 2)
        score_square(0, 3)
        quantise_values(0, 1, 0, 2)
        regroup_values(0, 1, 2, 2, FIRST_REGROUP[3])
        quantise_scores(0, 1)
        quantise_values(0, 1, 2, 2)
        regroup_values(1, 0)
        linear_attention(0)
        linear_attention(1)
        transpose_tokens(1)

        for m in range(QUAD_LEAD):
            quadratic_attention(m)
        for t in range(4):
            score_relu(1, t)
        for n in range(0, SLOTS + PROJECT_LAG):
            if n % SLOTS_PER_CHUNK == 0:
                c = n // SLOTS_PER_CHUNK
                load_gate(c + 1)
                load_tokens(c + 3)
                load_values(c + 3)
            if n == 19:
                sort_kv(1, 0)
            if n == 23:
                sort_kv(1, 1)
            quadratic_attention(n + QUAD_LEAD)
            add_quadratic(n)
            gate(n - GATE_LAG)
            if n == SLOTS:
                quantise_hidden(SLOTS // PERIOD)
            project(n - PROJECT_LAG)
            lin_slot = n + LIN_LEAD if n > 0 else HALVES
            if lin_slot % HALVES == 0:
                linear_attention(lin_slot)
            transpose_gate(n - GATE_T_LAG)
            if (n + TOKENS_LEAD) % SLOTS_PER_CHUNK == 0 and n + TOKENS_LEAD >= 2 * SLOTS_PER_CHUNK:
                transpose_tokens((n + TOKENS_LEAD) // SLOTS_PER_CHUNK)
            if lin_slot % HALVES == 0:
                linear_attention(lin_slot + 1)
            for piece in {0: (4,), 1: (5,), 2: (6,), 3: (7,)}.get(n, ()):
                scores(SLOTS_PER_CHUNK + piece)
            if n + PREPARE_LEAD >= 2 * SLOTS_PER_CHUNK:
                scores(n + PREPARE_LEAD)
            if n % PERIOD == PERIOD - 1 and n < SLOTS:
                period = n // PERIOD
                c, half = divmod(period + 2, HALVES)
                quantise_hidden(period)
                quantise_scores(c, half)
                quantise_values(c, half)
                regroup_values((period + 3) // HALVES, (period + 3) % HALVES)
            if n % PERIOD == PERIOD - 1 and n > PERIOD:
                add_bias_and_store(n - PROJECT_LAG - 3)
                add_bias_and_store(n - PROJECT_LAG - 1)
